import numpy as np
import ml_dtypes


def mxq(x, axis, fmt="e4m3"):
    dtype, down = {"e4m3": (ml_dtypes.float8_e4m3fn, 7), "e5m2": (ml_dtypes.float8_e5m2, 14)}[fmt]
    v = np.moveaxis(np.asarray(x, np.float32).astype(ml_dtypes.bfloat16).astype(np.float64), axis, -1)
    blocks = v.reshape(v.shape[:-1] + (-1, 32))
    amax = np.abs(blocks).max(-1, keepdims=True)
    byte = np.maximum(np.where(amax > 0, np.frexp(amax)[1] - 1 + 127, 0) - down, 1)
    scale = np.exp2(byte - 127.0)
    codes = (blocks / scale).astype(np.float32).astype(dtype).astype(np.float64)
    return np.moveaxis((codes * scale).reshape(v.shape), -1, axis)


WIDE = False


def mx_kscale(k):
    if not WIDE:
        return np.ones(k)
    levels = np.array([10, -10, 5, -5, 0])
    if k % 512:
        return np.exp2(np.random.permutation(np.resize(levels, k // 32))).repeat(32)
    a = np.empty((k // 512, 16))
    for p in range(k // 512):
        a[p, :8] = np.random.permutation(np.resize(levels, 8))
        for g in range(8):
            far = levels[np.abs(levels - a[p, g]) >= 10]
            a[p, g + 8] = far[np.random.randint(len(far))]
    return np.exp2(a.ravel()).repeat(32)


BF16 = ml_dtypes.bfloat16


def bf(x):
    return np.asarray(x, np.float32).astype(BF16)


def f64(x):
    return np.asarray(x).astype(np.float64)


B, C, CP, H, W, KW = 1, 512, 19, 48, 48, 7
PAD = KW // 2
BN_EPS = 1e-5


def pad_hw(v):
    return np.pad(v, ((0, 0), (0, 0), (PAD, PAD), (PAD, PAD)))


def setup_inputs():
    s, t = mx_kscale(C), mx_kscale(C)
    return {
        "x": bf(np.random.standard_normal((B, C, H, W))),
        "coarse_probs": bf(np.random.random((B, CP, H, W))),
        "sigma": bf(1.5 + 0.1 * np.random.standard_normal(1)),
        "w_feat": bf(np.random.standard_normal((C, C)) * 2.0 / np.sqrt(C) * t[:, None] / s[None, :]),
        "w_fuse": bf(np.random.standard_normal((C, C)) * 2.5 / np.sqrt(C) / t[None, :]),
        "bn_gamma": bf((1.0 + 0.1 * np.random.standard_normal(C)) * s),
        "bn_beta": bf(0.1 * np.random.standard_normal(C) * s),
        "bn_mean": bf(0.1 * np.random.standard_normal(C)),
        "bn_var": bf(np.random.random(C) + 0.5),
    }


def reference(x, coarse_probs, sigma, w_feat, w_fuse, bn_gamma, bn_beta, bn_mean, bn_var):
    x, p = f64(x), f64(coarse_probs)
    inv = 1.0 / np.sqrt(f64(bn_var) + BN_EPS)
    xn = (x - f64(bn_mean)[None, :, None, None]) * (inv * f64(bn_gamma))[None, :, None, None] + f64(bn_beta)[None, :, None, None]

    pp = pad_hw(p)
    dist_sq = np.stack([((pp[:, :, i:i + H, j:j + W] - p) ** 2).sum(axis=1) for i in range(KW) for j in range(KW)], axis=1)
    denom = 2.0 * np.maximum(f64(sigma)[0], 0.0) ** 2 + 1e-8
    a = np.exp(-dist_sq / denom)
    e = np.exp(a - a.max(axis=1, keepdims=True))
    affinity = e / e.sum(axis=1, keepdims=True)

    xq = mxq(xn, 1, "e4m3")
    messages = f64(bf(mxq(f64(w_feat), 1, "e4m3") @ xq.reshape(B, C, H * W))).reshape(B, C, H, W)

    mp = pad_hw(messages)
    agg = np.zeros((B, C, H, W))
    for i in range(KW):
        for j in range(KW):
            agg = agg + mp[:, :, i:i + H, j:j + W] * affinity[:, i * KW + j][:, None]

    aq = mxq(agg, 1, "e4m3")
    refined = (mxq(f64(w_fuse), 1, "e4m3") @ aq.reshape(B, C, H * W)).reshape(B, C, H, W)
    return x + refined

@@ -1,0 +1,342 @@
+from contextlib import ExitStack
+
+import concourse.masks as masks
+import concourse.mybir as mybir
+
+F32 = mybir.dt.float32
+BF16 = mybir.dt.bfloat16
+U32 = mybir.dt.uint32
+U8 = mybir.dt.uint8
+I32 = mybir.dt.int32
+FP8X4 = mybir.dt.float8_e4m3fn_x4
+ALU = mybir.AluOpType
+ACT = mybir.ActivationFunctionType
+AX = mybir.AxisListType
+
+P = 128
+C = 512
+CP = 19
+IMG_W = 48
+HW = 2304
+KW = 7
+NOFF = 49
+PAIRS = 9
+PADM = 160
+ML = HW + 2 * PADM
+PADP = 4
+PL = HW + 2 * PADP
+MSG_DT = BF16
+G_COUNT = 17
+FLOPS = 2 * 2 * C * C * HW + 2 * NOFF * C * HW + 3 * NOFF * CP * HW
+
+
+def tile_dcblock_kernel(tc, x, coarse_probs, sigma, w_feat, w_fuse, bn_gamma, bn_beta, bn_mean, bn_var, out):
+    nc = tc.nc
+    x_v = x[0].rearrange("(p j) h w -> p j (h w)", j=4)
+    out_v = out[0].rearrange("(m t) h w -> m t (h w)", t=4)
+    cp_v = coarse_probs[0].rearrange("c h w -> c (h w)")
+    g_set = set(i for i in range(NOFF) if ((i + 1) * G_COUNT) // NOFF > (i * G_COUNT) // NOFF)
+
+    with ExitStack() as ctx:
+        const = ctx.enter_context(tc.tile_pool(name="const", bufs=1))
+        work = ctx.enter_context(tc.tile_pool(name="work", bufs=2))
+        affp = ctx.enter_context(tc.tile_pool(name="affp", bufs=2))
+        accp = ctx.enter_context(tc.tile_pool(name="accp", bufs=4))
+        ps_win = ctx.enter_context(tc.psum_pool(name="ps_win", bufs=5))
+        ps_aux = ctx.enter_context(tc.psum_pool(name="ps_aux", bufs=3))
+
+        x_raw = const.tile([P, 4, HW], BF16, name="x_raw")
+        wf_raw = const.tile([P, 4, C], BF16, name="wf_raw")
+        wu_raw = const.tile([P, 4, C], BF16, name="wu_raw")
+        chunks = [(0, 512), (512, 512), (1024, 512), (1536, 512), (2048, 256)]
+        nc.sync.dma_start(out=x_raw[:, :, 0:512], in_=x_v[:, :, 0:512])
+        nc.sync.dma_start(out=wf_raw[:], in_=w_feat.rearrange("(m t) k -> m t k", t=4))
+        for c0, wd in chunks[1:]:
+            nc.sync.dma_start(out=x_raw[:, :, c0:c0 + wd], in_=x_v[:, :, c0:c0 + wd])
+        nc.sync.dma_start(out=wu_raw[:], in_=w_fuse.rearrange("(m t) k -> m t k", t=4))
+
+        gam = const.tile([P, 4], BF16, name="gam")
+        bet = const.tile([P, 4], BF16, name="bet")
+        mea = const.tile([P, 4], BF16, name="mea")
+        var = const.tile([P, 4], BF16, name="var")
+        sig = const.tile([P, 1], BF16, name="sig")
+        nc.scalar.dma_start(out=var[:], in_=bn_var.rearrange("(p j) -> p j", j=4))
+        nc.scalar.dma_start(out=gam[:], in_=bn_gamma.rearrange("(p j) -> p j", j=4))
+        nc.scalar.dma_start(out=mea[:], in_=bn_mean.rearrange("(p j) -> p j", j=4))
+        nc.scalar.dma_start(out=bet[:], in_=bn_beta.rearrange("(p j) -> p j", j=4))
+        nc.scalar.dma_start(out=sig[:], in_=sigma.partition_broadcast(P))
+
+        pk_a = const.tile([P, PL], BF16, name="pk_a")
+        pk_b = const.tile([P, PL], BF16, name="pk_b")
+        nc.vector.memset(pk_a[:], 0.0)
+        nc.gpsimd.memset(pk_b[:], 0.0)
+        for dix in range(KW):
+            di = dix - 3
+            pk = pk_a if dix < 4 else pk_b
+            s = dix if dix < 4 else dix - 4
+            q_lo = max(0, PADP - IMG_W * di)
+            q_hi = min(PL, HW + PADP - IMG_W * di)
+            nc.scalar.dma_start(
+                out=pk[CP * s:CP * s + CP, q_lo:q_hi],
+                in_=cp_v[:, q_lo - PADP + IMG_W * di:q_hi - PADP + IMG_W * di],
+            )
+
+        ident_f = const.tile([P, P], F32, name="ident_f")
+        masks.make_identity(nc, ident_f[:])
+        ident_b = const.tile([P, P], BF16, name="ident_b")
+        masks.make_identity(nc, ident_b[:])
+        ident_w = ident_b
+
+        msg = const.tile([P, 4, ML], MSG_DT, name="msg")
+        nc.gpsimd.memset(msg[:, :, 0:PADM], 0.0)
+        nc.gpsimd.memset(msg[:, :, PADM + HW:ML], 0.0)
+
+        v1 = const.tile([P, 4], F32, name="v1")
+        nc.vector.tensor_scalar_add(out=v1[:], in0=var[:], scalar1=1e-5)
+        sq = const.tile([P, 4], F32, name="sq")
+        nc.scalar.activation(out=sq[:], in_=v1[:], func=ACT.Sqrt)
+        r0 = const.tile([P, 4], F32, name="r0")
+        nc.vector.reciprocal(out=r0[:], in_=sq[:])
+        nt = const.tile([P, 4], F32, name="nt")
+        nc.vector.tensor_tensor(out=nt[:], in0=r0[:], in1=r0[:], op=ALU.mult)
+        nc.vector.tensor_tensor(out=nt[:], in0=nt[:], in1=v1[:], op=ALU.mult)
+        nc.vector.tensor_scalar(out=nt[:], in0=nt[:], scalar1=-0.5, scalar2=1.5, op0=ALU.mult, op1=ALU.add)
+        nc.vector.tensor_tensor(out=nt[:], in0=nt[:], in1=r0[:], op=ALU.mult)
+        bn_s = const.tile([P, 4], F32, name="bn_s")
+        nc.vector.tensor_tensor(out=bn_s[:], in0=nt[:], in1=gam[:], op=ALU.mult)
+        bn_b = const.tile([P, 4], F32, name="bn_b")
+        nc.vector.tensor_tensor(out=bn_b[:], in0=bn_s[:], in1=mea[:], op=ALU.mult)
+        nc.vector.tensor_tensor(out=bn_b[:], in0=bet[:], in1=bn_b[:], op=ALU.subtract)
+
+        sg = const.tile([P, 1], F32, name="sg")
+        nc.vector.tensor_scalar_max(out=sg[:], in0=sig[:], scalar1=0.0)
+        nc.vector.tensor_tensor(out=sg[:], in0=sg[:], in1=sg[:], op=ALU.mult)
+        nc.vector.tensor_scalar(out=sg[:], in0=sg[:], scalar1=2.0, scalar2=1e-8, op0=ALU.mult, op1=ALU.add)
+        neginv = const.tile([P, 1], F32, name="neginv")
+        nc.vector.reciprocal(out=neginv[:], in_=sg[:])
+        nc.vector.tensor_scalar_mul(out=neginv[:], in0=neginv[:], scalar1=-1.0)
+
+        NT = 2 * PAIRS
+        n_i = const.tile([P, NT], I32, name="n_i")
+        nc.gpsimd.iota(n_i[:], pattern=[[P, NT]], base=0, channel_multiplier=1)
+        thr_i = const.tile([P, IMG_W - 1], I32, name="thr_i")
+        nc.gpsimd.iota(thr_i[:], pattern=[[IMG_W, IMG_W - 1]], base=IMG_W, channel_multiplier=0)
+        dj_i = const.tile([P, KW], I32, name="dj_i")
+        nc.gpsimd.iota(dj_i[:], pattern=[[1, KW]], base=-3, channel_multiplier=0)
+        n_f = const.tile([P, NT], F32, name="n_f")
+        nc.vector.tensor_copy(out=n_f[:], in_=n_i[:])
+        thr_f = const.tile([P, IMG_W - 1], F32, name="thr_f")
+        nc.vector.tensor_copy(out=thr_f[:], in_=thr_i[:])
+        dj_f = const.tile([P, KW], F32, name="dj_f")
+        nc.vector.tensor_copy(out=dj_f[:], in_=dj_i[:])
+        cmp = const.tile([P, NT, IMG_W - 1], F32, name="cmp")
+        nc.vector.tensor_tensor(
+            out=cmp[:],
+            in0=n_f[:].unsqueeze(2).to_broadcast([P, NT, IMG_W - 1]),
+            in1=thr_f[:].unsqueeze(1).to_broadcast([P, NT, IMG_W - 1]),
+            op=ALU.is_ge,
+        )
+        row = const.tile([P, NT], F32, name="row")
+        nc.vector.tensor_reduce(out=row[:], in_=cmp[:], axis=AX.X, op=ALU.add)
+        col = const.tile([P, NT], F32, name="col")
+        nc.vector.scalar_tensor_tensor(out=col[:], in0=row[:], scalar=-48.0, in1=n_f[:], op0=ALU.mult, op1=ALU.add)
+        cj = const.tile([P, NT, KW], F32, name="cj")
+        nc.vector.tensor_tensor(
+            out=cj[:],
+            in0=col[:].unsqueeze(2).to_broadcast([P, NT, KW]),
+            in1=dj_f[:].unsqueeze(1).to_broadcast([P, NT, KW]),
+            op=ALU.add,
+        )
+        m_lo = const.tile([P, NT, KW], F32, name="m_lo")
+        nc.vector.tensor_scalar(out=m_lo[:], in0=cj[:], scalar1=0.0, scalar2=None, op0=ALU.is_ge)
+        mask7 = const.tile([P, NT, KW], F32, name="mask7")
+        nc.vector.scalar_tensor_tensor(
+            out=mask7[:].rearrange("p t j -> p (t j)"),
+            in0=cj[:].rearrange("p t j -> p (t j)"),
+            scalar=47.0,
+            in1=m_lo[:].rearrange("p t j -> p (t j)"),
+            op0=ALU.is_le,
+            op1=ALU.mult,
+        )
+        cnt = const.tile([P, NT], F32, name="cnt")
+        nc.vector.tensor_reduce(out=cnt[:], in_=mask7[:], axis=AX.X, op=ALU.add)
+        nc.vector.tensor_scalar(out=cnt[:], in0=cnt[:], scalar1=-7.0, scalar2=49.0, op0=ALU.mult, op1=ALU.add)
+        mask49 = const.tile([P, NT, KW, KW], F32, name="mask49")
+        nc.vector.tensor_copy(out=mask49[:], in_=mask7[:].unsqueeze(3).to_broadcast([P, NT, KW, KW]))
+
+        def prep_weight(raw, label):
+            grouped = const.tile([P, 4 * C], BF16, name=label + "_grouped", align_bytes=64)
+            gw = grouped[:].bitcast(F32).rearrange("p (t m u) -> p t m u", t=4, u=2)
+            for half in range(2):
+                ps = ps_aux.tile([P, 2, 2, P], F32, name=label + "_ps", tag="aux")
+                for tt in range(2):
+                    words = raw[:, 2 * half + tt, :].bitcast(F32)
+                    for u in range(2):
+                        nc.tensor.transpose(ps[:, tt, u, :], words[:, u::2], ident_f[:])
+                nc.vector.tensor_copy(out=gw[:, 2 * half:2 * half + 2], in_=ps[:].rearrange("p t u m -> p t m u"))
+            codes = const.tile([P, C], U32, name=label + "_codes", align_bytes=64)
+            scl = const.tile([P, C], U8, name=label + "_scl", align_bytes=64)
+            nc.vector.quantize_mx(out=codes[:].bitcast(FP8X4), scales=scl[:], in_=grouped[:])
+            return codes, scl
+
+        wf_codes, wf_scl = prep_weight(wf_raw, "wf")
+
+        x_codes = const.tile([P, HW], U32, name="x_codes", align_bytes=64)
+        x_scl = const.tile([P, HW], U8, name="x_scl", align_bytes=64)
+
+        def stage1(k):
+            c0, wd = chunks[k]
+            xn = work.tile([P, 4, wd], BF16, name="xn", tag="xn")
+            for j in range(4):
+                nc.scalar.activation(
+                    out=xn[:, j, :], in_=x_raw[:, j, c0:c0 + wd], func=ACT.Identity,
+                    scale=bn_s[:, j:j + 1], bias=bn_b[:, j:j + 1],
+                )
+            xg = work.tile([P, wd, 4], BF16, name="xg", tag="xg", align_bytes=64)
+            nc.vector.tensor_copy(out=xg[:], in_=xn[:].rearrange("p j n -> p n j"))
+            nc.vector.quantize_mx(
+                out=x_codes[:, c0:c0 + wd].bitcast(FP8X4), scales=x_scl[:, c0:c0 + wd],
+                in_=xg[:].rearrange("p n j -> p (n j)"),
+            )
+            for i in range(4 if wd == 512 else 2):
+                bank = ps_win.tile([P, 2, 256], MSG_DT, name="bank", tag="win")
+                for h in range(2):
+                    t = i if wd == 512 else 2 * i + h
+                    n0 = c0 + 256 * h if wd == 512 else c0
+                    nc.tensor.matmul_mx(
+                        out=bank[:, h, :],
+                        lhsT=wf_codes[:, P * t:P * t + P].bitcast(FP8X4), lhsT_scale=wf_scl[:, P * t:P * t + P],
+                        rhs=x_codes[:, n0:n0 + 256].bitcast(FP8X4), rhs_scale=x_scl[:, n0:n0 + 256],
+                        start=True, stop=True,
+                    )
+                if wd == 512:
+                    nc.scalar.copy(out=msg[:, i, PADM + c0:PADM + c0 + 512], in_=bank[:].rearrange("p h n -> p (h n)"))
+                else:
+                    nc.scalar.copy(out=msg[:, 2 * i:2 * i + 2, PADM + c0:PADM + c0 + 256], in_=bank[:])
+
+        def affinity(pi):
+            diff = affp.tile([P, 2, NOFF + 1, CP], F32, name="diff", tag="diff")
+            for a in range(2):
+                n0 = PADP + P * (2 * pi + a) - 3
+                win_a = ps_aux.tile([P, KW, P], BF16, name="win_a", tag="aux")
+                win_b = ps_aux.tile([P, KW, P], BF16, name="win_b", tag="aux")
+                for djx in range(KW):
+                    nc.tensor.transpose(win_a[:, djx, :], pk_a[:, n0 + djx:n0 + djx + P], ident_b[:])
+                for djx in range(KW):
+                    nc.tensor.transpose(win_b[:, djx, :], pk_b[:, n0 + djx:n0 + djx + P], ident_b[:])
+                nc.scalar.copy(out=diff[:, a, NOFF, :], in_=win_a[:, 3, 3 * CP:4 * CP])
+                dv = diff[:, a, 0:NOFF, :].rearrange("p (j i) c -> p j i c", i=KW)
+                centre = diff[:, a, NOFF:NOFF + 1, :].unsqueeze(1)
+                nc.vector.tensor_tensor(
+                    out=dv[:, :, 0:4, :], in0=win_a[:, :, 0:4 * CP].rearrange("p j (i c) -> p j i c", c=CP),
+                    in1=centre.to_broadcast([P, KW, 4, CP]), op=ALU.subtract,
+                )
+                nc.vector.tensor_tensor(
+                    out=dv[:, :, 4:7, :], in0=win_b[:, :, 0:3 * CP].rearrange("p j (i c) -> p j i c", c=CP),
+                    in1=centre.to_broadcast([P, KW, 3, CP]), op=ALU.subtract,
+                )
+            flat = diff[:].rearrange("p a f c -> p (a f c)")
+            nc.scalar.activation(out=flat, in_=flat, func=ACT.Square)
+            dist = affp.tile([P, 2 * (NOFF + 1)], F32, name="dist", tag="dist")
+            nc.vector.tensor_reduce(out=dist[:], in_=diff[:].rearrange("p a f c -> p (a f) c"), axis=AX.X, op=ALU.add)
+            gau = affp.tile([P, 2 * (NOFF + 1)], F32, name="gau", tag="gau")
+            nc.scalar.activation(out=gau[:], in_=dist[:], func=ACT.Exp, scale=neginv[:, 0:1])
+            ex = affp.tile([P, 2, NOFF + 1], F32, name="ex", tag="ex")
+            nc.scalar.activation(out=ex[:].rearrange("p a f -> p (a f)"), in_=gau[:], func=ACT.Exp, bias=-1.0)
+            em = affp.tile([P, 2, NOFF], F32, name="em", tag="em")
+            nc.vector.tensor_tensor(
+                out=em[:], in0=ex[:, :, 0:NOFF],
+                in1=mask49[:, 2 * pi:2 * pi + 2].rearrange("p t j i -> p t (j i)"), op=ALU.mult,
+            )
+            zs = affp.tile([P, 2], F32, name="zs", tag="zs")
+            nc.vector.tensor_reduce(out=zs[:], in_=em[:], axis=AX.X, op=ALU.add)
+            zo = affp.tile([P, 2], F32, name="zo", tag="zo")
+            nc.vector.tensor_tensor(out=zo[:], in0=ex[:, :, NOFF], in1=cnt[:, 2 * pi:2 * pi + 2], op=ALU.mult)
+            nc.vector.tensor_tensor(out=zo[:], in0=zo[:], in1=zs[:], op=ALU.add)
+            rz = affp.tile([P, 2], F32, name="rz", tag="rz")
+            nc.vector.reciprocal(out=rz[:], in_=zo[:])
+            wa = affp.tile([P, 2, NOFF], F32, name="wa", tag="wa", bufs=3)
+            nc.vector.tensor_tensor(out=wa[:], in0=em[:], in1=rz[:].unsqueeze(2).to_broadcast([P, 2, NOFF]), op=ALU.mult)
+            return wa
+
+        def aggregate(pi, wa):
+            acc_v0 = accp.tile([P, C], F32, name="acc_v0", tag="acc_v")
+            acc_v1 = accp.tile([P, C], F32, name="acc_v1", tag="acc_v")
+            acc_g0 = accp.tile([P, C], F32, name="acc_g0", tag="acc_g")
+            acc_g1 = accp.tile([P, C], F32, name="acc_g1", tag="acc_g")
+            acc_v = [acc_v0, acc_v1]
+            acc_g = [acc_g0, acc_g1]
+            seen_v = 0
+            seen_g = 0
+            for f in range(NOFF):
+                djx, dix = divmod(f, KW)
+                shift = IMG_W * (dix - 3) + (djx - 3)
+                for a in range(2):
+                    base = PADM + P * (2 * pi + a) + shift
+                    win = ps_win.tile([P, C], MSG_DT, name="win", tag="win")
+                    for t in range(4):
+                        nc.tensor.transpose(win[:, P * t:P * t + P], msg[:, t, base:base + P], ident_w[:])
+                    wcol = wa[:, a, f:f + 1]
+                    if f in g_set:
+                        if seen_g == 0:
+                            nc.scalar.activation(out=acc_g[a][:], in_=win[:], func=ACT.Copy, scale=wcol)
+                        else:
+                            prod = accp.tile([P, C], F32, name="prod", tag="prod")
+                            nc.scalar.activation(out=prod[:], in_=win[:], func=ACT.Copy, scale=wcol)
+                            nc.gpsimd.tensor_tensor(out=acc_g[a][:], in0=acc_g[a][:], in1=prod[:], op=ALU.add)
+                    else:
+                        if seen_v == 0:
+                            nc.vector.tensor_scalar(out=acc_v[a][:], in0=win[:], scalar1=wcol, scalar2=None, op0=ALU.mult)
+                        else:
+                            nc.vector.scalar_tensor_tensor(
+                                out=acc_v[a][:], in0=win[:], scalar=wcol, in1=acc_v[a][:], op0=ALU.mult, op1=ALU.add,
+                            )
+                if f in g_set:
+                    seen_g += 1
+                else:
+                    seen_v += 1
+            agg_t = work.tile([P, 2, C], BF16, name="agg_t", tag="agg_t")
+            for a in range(2):
+                nc.gpsimd.tensor_tensor(out=agg_t[:, a, :], in0=acc_g[a][:], in1=acc_v[a][:], op=ALU.add)
+            return agg_t
+
+        def stage2(pi, agg_t):
+            back = ps_aux.tile([P, 2, 4, P], BF16, name="back", tag="aux")
+            for a in range(2):
+                for t in range(4):
+                    nc.tensor.transpose(back[:, a, t, :], agg_t[:, a, P * t:P * t + P], ident_b[:])
+            ag = work.tile([P, 2 * P, 4], BF16, name="ag", tag="ag", align_bytes=64)
+            nc.scalar.copy(out=ag[:].rearrange("p (a n) t -> p a n t", a=2), in_=back[:].rearrange("p a t n -> p a n t"))
+            a_codes = work.tile([P, 2 * P], U32, name="a_codes", tag="a_codes", align_bytes=64)
+            a_scl = work.tile([P, 2 * P], U8, name="a_scl", tag="a_scl", align_bytes=64)
+            nc.vector.quantize_mx(out=a_codes[:].bitcast(FP8X4), scales=a_scl[:], in_=ag[:].rearrange("p n t -> p (n t)"))
+            o_sb = work.tile([P, 4, 2 * P], F32, name="o_sb", tag="o_sb", bufs=3)
+            n0 = 2 * P * pi
+            for u in range(2):
+                ps2 = ps_aux.tile([P, 2, 2 * P], F32, name="ps2", tag="aux")
+                for h in range(2):
+                    t = 2 * u + h
+                    nc.tensor.matmul_mx(
+                        out=ps2[:, h, :],
+                        lhsT=wu_codes[:, P * t:P * t + P].bitcast(FP8X4), lhsT_scale=wu_scl[:, P * t:P * t + P],
+                        rhs=a_codes[:].bitcast(FP8X4), rhs_scale=a_scl[:],
+                        start=True, stop=True,
+                    )
+                nc.vector.tensor_tensor(
+                    out=o_sb[:, 2 * u:2 * u + 2, :], in0=ps2[:], in1=x_raw[:, 2 * u:2 * u + 2, n0:n0 + 2 * P], op=ALU.add,
+                )
+            nc.sync.dma_start(out=out_v[:, :, n0:n0 + 2 * P], in_=o_sb[:])
+
+        stage1(0)
+        wa_next = affinity(0)
+        stage1(1)
+        wu_codes, wu_scl = prep_weight(wu_raw, "wu")
+        need = {1: 2, 3: 3, 5: 4}
+        for pi in range(PAIRS):
+            wa_now = wa_next
+            if pi in need:
+                stage1(need[pi])
+            if pi + 1 < PAIRS:
+                wa_next = affinity(pi + 1)
+            agg_t = aggregate(pi, wa_now)
+            stage2(pi, agg_t)

@@ -26,7 +26,7 @@ ML = HW + 2 * PADM
 PADP = 4
 PL = HW + 2 * PADP
 MSG_DT = BF16
-G_COUNT = 17
+G_COUNT = 20
 FLOPS = 2 * 2 * C * C * HW + 2 * NOFF * C * HW + 3 * NOFF * CP * HW
 
 
@@ -49,12 +49,13 @@ def tile_dcblock_kernel(tc, x, coarse_probs, sigma, w_feat, w_fuse, bn_gamma, bn
         wf_raw = const.tile([P, 4, C], BF16, name="wf_raw")
         wu_raw = const.tile([P, 4, C], BF16, name="wu_raw")
         chunks = [(0, 512), (512, 512), (1024, 512), (1536, 512), (2048, 256)]
-        nc.sync.dma_start(out=x_raw[:, :, 0:512], in_=x_v[:, :, 0:512])
-        nc.sync.dma_start(out=wf_raw[:], in_=w_feat.rearrange("(m t) k -> m t k", t=4))
-        for c0, wd in chunks[1:]:
-            nc.sync.dma_start(out=x_raw[:, :, c0:c0 + wd], in_=x_v[:, :, c0:c0 + wd])
-        nc.sync.dma_start(out=wu_raw[:], in_=w_fuse.rearrange("(m t) k -> m t k", t=4))
 
+        pk_a = const.tile([P, PL], BF16, name="pk_a")
+        pk_b = const.tile([P, PL], BF16, name="pk_b")
+        one = const.tile([P, 1], F32, name="one")
+        nc.vector.memset(one[:], 1.0)
+        nc.vector.memset(pk_a[:], 0.0)
+        nc.vector.memset(pk_b[:], 0.0)
         gam = const.tile([P, 4], BF16, name="gam")
         bet = const.tile([P, 4], BF16, name="bet")
         mea = const.tile([P, 4], BF16, name="mea")
@@ -66,20 +67,24 @@ def tile_dcblock_kernel(tc, x, coarse_probs, sigma, w_feat, w_fuse, bn_gamma, bn
         nc.scalar.dma_start(out=bet[:], in_=bn_beta.rearrange("(p j) -> p j", j=4))
         nc.scalar.dma_start(out=sig[:], in_=sigma.partition_broadcast(P))
 
-        pk_a = const.tile([P, PL], BF16, name="pk_a")
-        pk_b = const.tile([P, PL], BF16, name="pk_b")
-        nc.vector.memset(pk_a[:], 0.0)
-        nc.gpsimd.memset(pk_b[:], 0.0)
+        warm = const.tile([P, 1], F32, name="warm")
+        nc.scalar.activation(out=warm[:], in_=one[:], func=ACT.Sqrt)
         for dix in range(KW):
             di = dix - 3
             pk = pk_a if dix < 4 else pk_b
             s = dix if dix < 4 else dix - 4
             q_lo = max(0, PADP - IMG_W * di)
             q_hi = min(PL, HW + PADP - IMG_W * di)
-            nc.scalar.dma_start(
-                out=pk[CP * s:CP * s + CP, q_lo:q_hi],
-                in_=cp_v[:, q_lo - PADP + IMG_W * di:q_hi - PADP + IMG_W * di],
-            )
+            n_lo = q_lo - PADP + IMG_W * di
+            n_hi = q_hi - PADP + IMG_W * di
+            nc.sync.dma_start(out=pk[CP * s:CP * s + 16, q_lo:q_hi], in_=cp_v[0:16, n_lo:n_hi])
+            nc.scalar.dma_start(out=pk[CP * s + 16:CP * s + CP, q_lo:q_hi], in_=cp_v[16:CP, n_lo:n_hi])
+
+        nc.sync.dma_start(out=x_raw[:, :, 0:512], in_=x_v[:, :, 0:512])
+        nc.sync.dma_start(out=wf_raw[:], in_=w_feat.rearrange("(m t) k -> m t k", t=4))
+        for c0, wd in chunks[1:]:
+            nc.sync.dma_start(out=x_raw[:, :, c0:c0 + wd], in_=x_v[:, :, c0:c0 + wd])
+        nc.sync.dma_start(out=wu_raw[:], in_=w_fuse.rearrange("(m t) k -> m t k", t=4))
 
         ident_f = const.tile([P, P], F32, name="ident_f")
         masks.make_identity(nc, ident_f[:])
@@ -187,13 +192,22 @@ def tile_dcblock_kernel(tc, x, coarse_probs, sigma, w_feat, w_fuse, bn_gamma, bn
         def stage1(k):
             c0, wd = chunks[k]
             xn = work.tile([P, 4, wd], BF16, name="xn", tag="xn")
-            for j in range(4):
-                nc.scalar.activation(
-                    out=xn[:, j, :], in_=x_raw[:, j, c0:c0 + wd], func=ACT.Identity,
-                    scale=bn_s[:, j:j + 1], bias=bn_b[:, j:j + 1],
-                )
             xg = work.tile([P, wd, 4], BF16, name="xg", tag="xg", align_bytes=64)
-            nc.vector.tensor_copy(out=xg[:], in_=xn[:].rearrange("p j n -> p n j"))
+            for j in range(4):
+                if k == 0:
+                    nc.vector.tensor_scalar(
+                        out=xn[:, j, :], in0=x_raw[:, j, c0:c0 + wd],
+                        scalar1=bn_s[:, j:j + 1], scalar2=bn_b[:, j:j + 1], op0=ALU.mult, op1=ALU.add,
+                    )
+                else:
+                    nc.scalar.activation(
+                        out=xn[:, j, :], in_=x_raw[:, j, c0:c0 + wd], func=ACT.Identity,
+                        scale=bn_s[:, j:j + 1], bias=bn_b[:, j:j + 1],
+                    )
+            if k == 0:
+                nc.vector.tensor_copy(out=xg[:], in_=xn[:].rearrange("p j n -> p n j"))
+            else:
+                nc.scalar.copy(out=xg[:], in_=xn[:].rearrange("p j n -> p n j"))
             nc.vector.quantize_mx(
                 out=x_codes[:, c0:c0 + wd].bitcast(FP8X4), scales=x_scl[:, c0:c0 + wd],
                 in_=xg[:].rearrange("p n j -> p (n j)"),
@@ -244,33 +258,42 @@ def tile_dcblock_kernel(tc, x, coarse_probs, sigma, w_feat, w_fuse, bn_gamma, bn
             ex = affp.tile([P, 2, NOFF + 1], F32, name="ex", tag="ex")
             nc.scalar.activation(out=ex[:].rearrange("p a f -> p (a f)"), in_=gau[:], func=ACT.Exp, bias=-1.0)
             em = affp.tile([P, 2, NOFF], F32, name="em", tag="em")
-            nc.vector.tensor_tensor(
+            nc.gpsimd.tensor_tensor(
                 out=em[:], in0=ex[:, :, 0:NOFF],
                 in1=mask49[:, 2 * pi:2 * pi + 2].rearrange("p t j i -> p t (j i)"), op=ALU.mult,
             )
             zs = affp.tile([P, 2], F32, name="zs", tag="zs")
             nc.vector.tensor_reduce(out=zs[:], in_=em[:], axis=AX.X, op=ALU.add)
             zo = affp.tile([P, 2], F32, name="zo", tag="zo")
-            nc.vector.tensor_tensor(out=zo[:], in0=ex[:, :, NOFF], in1=cnt[:, 2 * pi:2 * pi + 2], op=ALU.mult)
-            nc.vector.tensor_tensor(out=zo[:], in0=zo[:], in1=zs[:], op=ALU.add)
+            for a in range(2):
+                nc.scalar.activation(
+                    out=zo[:, a:a + 1], in_=ex[:, a, NOFF:NOFF + 1], func=ACT.Identity,
+                    scale=cnt[:, 2 * pi + a:2 * pi + a + 1], bias=zs[:, a:a + 1],
+                )
             rz = affp.tile([P, 2], F32, name="rz", tag="rz")
             nc.vector.reciprocal(out=rz[:], in_=zo[:])
             wa = affp.tile([P, 2, NOFF], F32, name="wa", tag="wa", bufs=3)
-            nc.vector.tensor_tensor(out=wa[:], in0=em[:], in1=rz[:].unsqueeze(2).to_broadcast([P, 2, NOFF]), op=ALU.mult)
+            for a in range(2):
+                nc.scalar.activation(out=wa[:, a, :], in_=em[:, a, :], func=ACT.Copy, scale=rz[:, a:a + 1])
             return wa
 
-        def aggregate(pi, wa):
-            acc_v0 = accp.tile([P, C], F32, name="acc_v0", tag="acc_v")
-            acc_v1 = accp.tile([P, C], F32, name="acc_v1", tag="acc_v")
-            acc_g0 = accp.tile([P, C], F32, name="acc_g0", tag="acc_g")
-            acc_g1 = accp.tile([P, C], F32, name="acc_g1", tag="acc_g")
-            acc_v = [acc_v0, acc_v1]
+        def aggregate(pi, wa, hooks):
+            acc_v = accp.tile([P, 2, C], F32, name="acc_v", tag="acc_v")
+            acc_g0 = accp.tile([P, 2, C], F32, name="acc_g0", tag="acc_g")
+            acc_g1 = accp.tile([P, 2, C], F32, name="acc_g1", tag="acc_g")
             acc_g = [acc_g0, acc_g1]
             seen_v = 0
             seen_g = 0
             for f in range(NOFF):
+                for hook in hooks.get(f, []):
+                    hook()
                 djx, dix = divmod(f, KW)
                 shift = IMG_W * (dix - 3) + (djx - 3)
+                if f in g_set:
+                    if seen_g < 2:
+                        prod = acc_g[seen_g]
+                    else:
+                        prod = accp.tile([P, 2, C], F32, name="prod", tag="prod")
                 for a in range(2):
                     base = PADM + P * (2 * pi + a) + shift
                     win = ps_win.tile([P, C], MSG_DT, name="win", tag="win")
@@ -278,26 +301,23 @@ def tile_dcblock_kernel(tc, x, coarse_probs, sigma, w_feat, w_fuse, bn_gamma, bn
                         nc.tensor.transpose(win[:, P * t:P * t + P], msg[:, t, base:base + P], ident_w[:])
                     wcol = wa[:, a, f:f + 1]
                     if f in g_set:
-                        if seen_g == 0:
-                            nc.scalar.activation(out=acc_g[a][:], in_=win[:], func=ACT.Copy, scale=wcol)
-                        else:
-                            prod = accp.tile([P, C], F32, name="prod", tag="prod")
-                            nc.scalar.activation(out=prod[:], in_=win[:], func=ACT.Copy, scale=wcol)
-                            nc.gpsimd.tensor_tensor(out=acc_g[a][:], in0=acc_g[a][:], in1=prod[:], op=ALU.add)
+                        nc.scalar.activation(out=prod[:, a, :], in_=win[:], func=ACT.Copy, scale=wcol)
+                    elif seen_v == 0:
+                        nc.vector.tensor_scalar(out=acc_v[:, a, :], in0=win[:], scalar1=wcol, scalar2=None, op0=ALU.mult)
                     else:
-                        if seen_v == 0:
-                            nc.vector.tensor_scalar(out=acc_v[a][:], in0=win[:], scalar1=wcol, scalar2=None, op0=ALU.mult)
-                        else:
-                            nc.vector.scalar_tensor_tensor(
-                                out=acc_v[a][:], in0=win[:], scalar=wcol, in1=acc_v[a][:], op0=ALU.mult, op1=ALU.add,
-                            )
+                        nc.vector.scalar_tensor_tensor(
+                            out=acc_v[:, a, :], in0=win[:], scalar=wcol, in1=acc_v[:, a, :], op0=ALU.mult, op1=ALU.add,
+                        )
                 if f in g_set:
+                    if seen_g >= 2:
+                        tgt = acc_g[seen_g % 2]
+                        nc.gpsimd.tensor_tensor(out=tgt[:], in0=tgt[:], in1=prod[:], op=ALU.add)
                     seen_g += 1
                 else:
                     seen_v += 1
+            nc.gpsimd.tensor_tensor(out=acc_g0[:], in0=acc_g0[:], in1=acc_g1[:], op=ALU.add)
             agg_t = work.tile([P, 2, C], BF16, name="agg_t", tag="agg_t")
-            for a in range(2):
-                nc.gpsimd.tensor_tensor(out=agg_t[:, a, :], in0=acc_g[a][:], in1=acc_v[a][:], op=ALU.add)
+            nc.gpsimd.tensor_tensor(out=agg_t[:], in0=acc_g0[:], in1=acc_v[:], op=ALU.add)
             return agg_t
 
         def stage2(pi, agg_t):
@@ -318,7 +338,7 @@ def tile_dcblock_kernel(tc, x, coarse_probs, sigma, w_feat, w_fuse, bn_gamma, bn
                     t = 2 * u + h
                     nc.tensor.matmul_mx(
                         out=ps2[:, h, :],
-                        lhsT=wu_codes[:, P * t:P * t + P].bitcast(FP8X4), lhsT_scale=wu_scl[:, P * t:P * t + P],
+                        lhsT=later["wu"][0][:, P * t:P * t + P].bitcast(FP8X4), lhsT_scale=later["wu"][1][:, P * t:P * t + P],
                         rhs=a_codes[:].bitcast(FP8X4), rhs_scale=a_scl[:],
                         start=True, stop=True,
                     )
@@ -327,16 +347,25 @@ def tile_dcblock_kernel(tc, x, coarse_probs, sigma, w_feat, w_fuse, bn_gamma, bn
                 )
             nc.sync.dma_start(out=out_v[:, :, n0:n0 + 2 * P], in_=o_sb[:])
 
+        later = {}
+
+        def make_weights():
+            later["wu"] = prep_weight(wu_raw, "wu")
+
+        def make_affinity(pi):
+            later["wa"] = affinity(pi)
+
         stage1(0)
-        wa_next = affinity(0)
-        stage1(1)
-        wu_codes, wu_scl = prep_weight(wu_raw, "wu")
-        need = {1: 2, 3: 3, 5: 4}
+        make_affinity(0)
         for pi in range(PAIRS):
-            wa_now = wa_next
-            if pi in need:
-                stage1(need[pi])
+            wa_now = later["wa"]
+            hooks = {}
+            if pi == 0:
+                hooks[4] = [lambda: stage1(1)]
+                hooks[10] = [make_weights]
+            if pi in (1, 3, 5):
+                hooks[4] = [lambda k=(pi + 3) // 2: stage1(k)]
             if pi + 1 < PAIRS:
-                wa_next = affinity(pi + 1)
-            agg_t = aggregate(pi, wa_now)
+                hooks[16] = [lambda q=pi + 1: make_affinity(q)]
+            agg_t = aggregate(pi, wa_now, hooks)
             stage2(pi, agg_t)

@@ -26,7 +26,8 @@ ML = HW + 2 * PADM
 PADP = 4
 PL = HW + 2 * PADP
 MSG_DT = BF16
-G_COUNT = 20
+G_COUNT = 17
+X_COUNT = 5
 FLOPS = 2 * 2 * C * C * HW + 2 * NOFF * C * HW + 3 * NOFF * CP * HW
 
 
@@ -36,6 +37,8 @@ def tile_dcblock_kernel(tc, x, coarse_probs, sigma, w_feat, w_fuse, bn_gamma, bn
     out_v = out[0].rearrange("(m t) h w -> m t (h w)", t=4)
     cp_v = coarse_probs[0].rearrange("c h w -> c (h w)")
     g_set = set(i for i in range(NOFF) if ((i + 1) * G_COUNT) // NOFF > (i * G_COUNT) // NOFF)
+    rest = [i for i in range(NOFF) if i not in g_set]
+    x_set = set(rest[j] for j in range(len(rest)) if ((j + 1) * X_COUNT) // len(rest) > (j * X_COUNT) // len(rest))
 
     with ExitStack() as ctx:
         const = ctx.enter_context(tc.tile_pool(name="const", bufs=1))
@@ -55,7 +58,7 @@ def tile_dcblock_kernel(tc, x, coarse_probs, sigma, w_feat, w_fuse, bn_gamma, bn
         one = const.tile([P, 1], F32, name="one")
         nc.vector.memset(one[:], 1.0)
         nc.vector.memset(pk_a[:], 0.0)
-        nc.vector.memset(pk_b[:], 0.0)
+        nc.gpsimd.memset(pk_b[:], 0.0)
         gam = const.tile([P, 4], BF16, name="gam")
         bet = const.tile([P, 4], BF16, name="bet")
         mea = const.tile([P, 4], BF16, name="mea")
@@ -90,16 +93,19 @@ def tile_dcblock_kernel(tc, x, coarse_probs, sigma, w_feat, w_fuse, bn_gamma, bn
         masks.make_identity(nc, ident_f[:])
         ident_b = const.tile([P, P], BF16, name="ident_b")
         masks.make_identity(nc, ident_b[:])
-        ident_w = ident_b
 
-        msg = const.tile([P, 4, ML], MSG_DT, name="msg")
-        nc.gpsimd.memset(msg[:, :, 0:PADM], 0.0)
-        nc.gpsimd.memset(msg[:, :, PADM + HW:ML], 0.0)
+        msg_e = const.tile([P, 4, ML], MSG_DT, name="msg_e")
+        msg_o = const.tile([P, 4, ML], MSG_DT, name="msg_o")
+        nc.gpsimd.memset(msg_e[:, :, 0:PADM], 0.0)
+        nc.gpsimd.memset(msg_e[:, :, PADM + HW:ML], 0.0)
+        nc.gpsimd.memset(msg_o[:, :, 0:PADM], 0.0)
+        nc.gpsimd.memset(msg_o[:, :, PADM + HW - 1:ML], 0.0)
 
         v1 = const.tile([P, 4], F32, name="v1")
         nc.vector.tensor_scalar_add(out=v1[:], in0=var[:], scalar1=1e-5)
         sq = const.tile([P, 4], F32, name="sq")
         nc.scalar.activation(out=sq[:], in_=v1[:], func=ACT.Sqrt)
+        nc.scalar.activation(out=warm[:], in_=one[:], func=ACT.Exp)
         r0 = const.tile([P, 4], F32, name="r0")
         nc.vector.reciprocal(out=r0[:], in_=sq[:])
         nt = const.tile([P, 4], F32, name="nt")
@@ -123,7 +129,7 @@ def tile_dcblock_kernel(tc, x, coarse_probs, sigma, w_feat, w_fuse, bn_gamma, bn
 
         NT = 2 * PAIRS
         n_i = const.tile([P, NT], I32, name="n_i")
-        nc.gpsimd.iota(n_i[:], pattern=[[P, NT]], base=0, channel_multiplier=1)
+        nc.gpsimd.iota(n_i[:], pattern=[[2 * P, PAIRS], [1, 2]], base=0, channel_multiplier=2)
         thr_i = const.tile([P, IMG_W - 1], I32, name="thr_i")
         nc.gpsimd.iota(thr_i[:], pattern=[[IMG_W, IMG_W - 1]], base=IMG_W, channel_multiplier=0)
         dj_i = const.tile([P, KW], I32, name="dj_i")
@@ -191,8 +197,8 @@ def tile_dcblock_kernel(tc, x, coarse_probs, sigma, w_feat, w_fuse, bn_gamma, bn
 
         def stage1(k):
             c0, wd = chunks[k]
-            xn = work.tile([P, 4, wd], BF16, name="xn", tag="xn")
-            xg = work.tile([P, wd, 4], BF16, name="xg", tag="xg", align_bytes=64)
+            xn = work.tile([P, 4, wd], BF16, name="xn", tag="xn", bufs=1)
+            xg = work.tile([P, wd, 4], BF16, name="xg", tag="xg", align_bytes=64, bufs=1)
             for j in range(4):
                 if k == 0:
                     nc.vector.tensor_scalar(
@@ -224,20 +230,22 @@ def tile_dcblock_kernel(tc, x, coarse_probs, sigma, w_feat, w_fuse, bn_gamma, bn
                         start=True, stop=True,
                     )
                 if wd == 512:
-                    nc.scalar.copy(out=msg[:, i, PADM + c0:PADM + c0 + 512], in_=bank[:].rearrange("p h n -> p (h n)"))
+                    nc.scalar.copy(out=msg_e[:, i, PADM + c0:PADM + c0 + 512], in_=bank[:].rearrange("p h n -> p (h n)"))
+                    nc.scalar.copy(out=msg_o[:, i, PADM + c0 - 1:PADM + c0 + 511], in_=bank[:].rearrange("p h n -> p (h n)"))
                 else:
-                    nc.scalar.copy(out=msg[:, 2 * i:2 * i + 2, PADM + c0:PADM + c0 + 256], in_=bank[:])
+                    nc.scalar.copy(out=msg_e[:, 2 * i:2 * i + 2, PADM + c0:PADM + c0 + 256], in_=bank[:])
+                    nc.scalar.copy(out=msg_o[:, 2 * i:2 * i + 2, PADM + c0 - 1:PADM + c0 + 255], in_=bank[:])
 
         def affinity(pi):
             diff = affp.tile([P, 2, NOFF + 1, CP], F32, name="diff", tag="diff")
             for a in range(2):
-                n0 = PADP + P * (2 * pi + a) - 3
+                n0 = PADP + 2 * P * pi + a - 3
                 win_a = ps_aux.tile([P, KW, P], BF16, name="win_a", tag="aux")
                 win_b = ps_aux.tile([P, KW, P], BF16, name="win_b", tag="aux")
                 for djx in range(KW):
-                    nc.tensor.transpose(win_a[:, djx, :], pk_a[:, n0 + djx:n0 + djx + P], ident_b[:])
+                    nc.tensor.transpose(win_a[:, djx, :], pk_a[:, n0 + djx:n0 + djx + 2 * P:2], ident_b[:])
                 for djx in range(KW):
-                    nc.tensor.transpose(win_b[:, djx, :], pk_b[:, n0 + djx:n0 + djx + P], ident_b[:])
+                    nc.tensor.transpose(win_b[:, djx, :], pk_b[:, n0 + djx:n0 + djx + 2 * P:2], ident_b[:])
                 nc.scalar.copy(out=diff[:, a, NOFF, :], in_=win_a[:, 3, 3 * CP:4 * CP])
                 dv = diff[:, a, 0:NOFF, :].rearrange("p (j i) c -> p j i c", i=KW)
                 centre = diff[:, a, NOFF:NOFF + 1, :].unsqueeze(1)
@@ -278,10 +286,11 @@ def tile_dcblock_kernel(tc, x, coarse_probs, sigma, w_feat, w_fuse, bn_gamma, bn
             return wa
 
         def aggregate(pi, wa, hooks):
-            acc_v = accp.tile([P, 2, C], F32, name="acc_v", tag="acc_v")
+            acc_v = accp.tile([P, 2, C], F32, name="acc_v", tag="acc_v", bufs=3)
             acc_g0 = accp.tile([P, 2, C], F32, name="acc_g0", tag="acc_g")
             acc_g1 = accp.tile([P, 2, C], F32, name="acc_g1", tag="acc_g")
             acc_g = [acc_g0, acc_g1]
+            parts = []
             seen_v = 0
             seen_g = 0
             for f in range(NOFF):
@@ -289,48 +298,62 @@ def tile_dcblock_kernel(tc, x, coarse_probs, sigma, w_feat, w_fuse, bn_gamma, bn
                     hook()
                 djx, dix = divmod(f, KW)
                 shift = IMG_W * (dix - 3) + (djx - 3)
+                if f in x_set:
+                    prod = accp.tile([P, 2, C], F32, name="xprod", tag="xprod", bufs=X_COUNT + 3)
+                    parts.append(prod)
                 if f in g_set:
                     if seen_g < 2:
                         prod = acc_g[seen_g]
                     else:
-                        prod = accp.tile([P, 2, C], F32, name="prod", tag="prod")
+                        prod = accp.tile([P, 2, C], F32, name="prod", tag="prod", bufs=3)
+                base = PADM + 2 * P * pi + shift
+                src = msg_e if base % 2 == 0 else msg_o
+                word0 = base // 2
+                win = ps_win.tile([P, C], F32, name="win", tag="win")
+                for t in range(4):
+                    nc.tensor.transpose(win[:, P * t:P * t + P], src[:, t, :].bitcast(F32)[:, word0:word0 + P], ident_f[:])
+                halves = win[:].bitcast(BF16)
                 for a in range(2):
-                    base = PADM + P * (2 * pi + a) + shift
-                    win = ps_win.tile([P, C], MSG_DT, name="win", tag="win")
-                    for t in range(4):
-                        nc.tensor.transpose(win[:, P * t:P * t + P], msg[:, t, base:base + P], ident_w[:])
                     wcol = wa[:, a, f:f + 1]
-                    if f in g_set:
-                        nc.scalar.activation(out=prod[:, a, :], in_=win[:], func=ACT.Copy, scale=wcol)
+                    if f in g_set or f in x_set:
+                        nc.scalar.activation(out=prod[:, a, :], in_=halves[:, a::2], func=ACT.Copy, scale=wcol)
                     elif seen_v == 0:
-                        nc.vector.tensor_scalar(out=acc_v[:, a, :], in0=win[:], scalar1=wcol, scalar2=None, op0=ALU.mult)
+                        nc.vector.tensor_scalar(out=acc_v[:, a, :], in0=halves[:, a::2], scalar1=wcol, scalar2=None, op0=ALU.mult)
                     else:
                         nc.vector.scalar_tensor_tensor(
-                            out=acc_v[:, a, :], in0=win[:], scalar=wcol, in1=acc_v[:, a, :], op0=ALU.mult, op1=ALU.add,
+                            out=acc_v[:, a, :], in0=halves[:, a::2], scalar=wcol, in1=acc_v[:, a, :], op0=ALU.mult, op1=ALU.add,
                         )
                 if f in g_set:
                     if seen_g >= 2:
                         tgt = acc_g[seen_g % 2]
                         nc.gpsimd.tensor_tensor(out=tgt[:], in0=tgt[:], in1=prod[:], op=ALU.add)
                     seen_g += 1
-                else:
+                elif f not in x_set:
                     seen_v += 1
-            nc.gpsimd.tensor_tensor(out=acc_g0[:], in0=acc_g0[:], in1=acc_g1[:], op=ALU.add)
-            agg_t = work.tile([P, 2, C], BF16, name="agg_t", tag="agg_t")
-            nc.gpsimd.tensor_tensor(out=agg_t[:], in0=acc_g0[:], in1=acc_v[:], op=ALU.add)
-            return agg_t
+            return parts + [acc_g0, acc_g1, acc_v]
 
-        def stage2(pi, agg_t):
-            back = ps_aux.tile([P, 2, 4, P], BF16, name="back", tag="aux")
-            for a in range(2):
-                for t in range(4):
-                    nc.tensor.transpose(back[:, a, t, :], agg_t[:, a, P * t:P * t + P], ident_b[:])
-            ag = work.tile([P, 2 * P, 4], BF16, name="ag", tag="ag", align_bytes=64)
-            nc.scalar.copy(out=ag[:].rearrange("p (a n) t -> p a n t", a=2), in_=back[:].rearrange("p a t n -> p a n t"))
+        def turn_back(parts, held, a, t):
+            if a == 0 and t == 0:
+                held["ag"] = work.tile([P, 2 * P, 4], BF16, name="ag", tag="ag", align_bytes=64)
+            if t == 0:
+                held["back"] = ps_aux.tile([P, 4, P], F32, name="back", tag="aux")
+            back = held["back"]
+            for i in range(len(parts)):
+                nc.tensor.matmul(
+                    out=back[:, t, :], lhsT=parts[i][:, a, P * t:P * t + P], rhs=ident_f[:],
+                    is_transpose=True, start=(i == 0), stop=(i == len(parts) - 1),
+                )
+            if t == 3:
+                nc.scalar.copy(
+                    out=held["ag"][:].rearrange("p (n a) t -> p a n t", a=2)[:, a], in_=back[:].rearrange("p t n -> p n t"),
+                )
+
+        def stage2(pi, held):
+            ag = held["ag"]
             a_codes = work.tile([P, 2 * P], U32, name="a_codes", tag="a_codes", align_bytes=64)
             a_scl = work.tile([P, 2 * P], U8, name="a_scl", tag="a_scl", align_bytes=64)
             nc.vector.quantize_mx(out=a_codes[:].bitcast(FP8X4), scales=a_scl[:], in_=ag[:].rearrange("p n t -> p (n t)"))
-            o_sb = work.tile([P, 4, 2 * P], F32, name="o_sb", tag="o_sb", bufs=3)
+            o_sb = work.tile([P, 4, 2 * P], F32, name="o_sb", tag="o_sb")
             n0 = 2 * P * pi
             for u in range(2):
                 ps2 = ps_aux.tile([P, 2, 2 * P], F32, name="ps2", tag="aux")
@@ -357,6 +380,7 @@ def tile_dcblock_kernel(tc, x, coarse_probs, sigma, w_feat, w_fuse, bn_gamma, bn
 
         stage1(0)
         make_affinity(0)
+        before = None
         for pi in range(PAIRS):
             wa_now = later["wa"]
             hooks = {}
@@ -364,8 +388,16 @@ def tile_dcblock_kernel(tc, x, coarse_probs, sigma, w_feat, w_fuse, bn_gamma, bn
                 hooks[4] = [lambda: stage1(1)]
                 hooks[10] = [make_weights]
             if pi in (1, 3, 5):
-                hooks[4] = [lambda k=(pi + 3) // 2: stage1(k)]
+                hooks[18] = [lambda k=(pi + 3) // 2: stage1(k)]
+            if before is not None:
+                held = {}
+                for i in range(8):
+                    hooks[2 * i + 1] = [lambda pp=before, hh=held, a=i // 4, t=i % 4: turn_back(pp, hh, a, t)]
+                hooks[17] = [lambda q=pi - 1, hh=held: stage2(q, hh)]
             if pi + 1 < PAIRS:
-                hooks[16] = [lambda q=pi + 1: make_affinity(q)]
-            agg_t = aggregate(pi, wa_now, hooks)
-            stage2(pi, agg_t)
+                hooks[20] = [lambda q=pi + 1: make_affinity(q)]
+            before = aggregate(pi, wa_now, hooks)
+        held = {}
+        for i in range(8):
+            turn_back(before, held, i // 4, i % 4)
+        stage2(PAIRS - 1, held)

@@ -20,14 +20,19 @@ IMG_W = 48
 HW = 2304
 KW = 7
 NOFF = 49
-PAIRS = 9
-PADM = 160
-ML = HW + 2 * PADM
+PE_PIX = 1792
+E_PAIRS = (7, 8)
+ME0 = 1536
+ML = 928
 PADP = 4
 PL = HW + 2 * PADP
-MSG_DT = BF16
-G_COUNT = 17
-X_COUNT = 5
+PK0 = 1784
+PKW = 528
+PITCH = 54
+PLW = 918
+NPOS = 24
+E_SPAN = 68
+G_COUNT = 16
 FLOPS = 2 * 2 * C * C * HW + 2 * NOFF * C * HW + 3 * NOFF * CP * HW
 
 
@@ -36,29 +41,29 @@ def tile_dcblock_kernel(tc, x, coarse_probs, sigma, w_feat, w_fuse, bn_gamma, bn
     x_v = x[0].rearrange("(p j) h w -> p j (h w)", j=4)
     out_v = out[0].rearrange("(m t) h w -> m t (h w)", t=4)
     cp_v = coarse_probs[0].rearrange("c h w -> c (h w)")
+    cp_r = coarse_probs[0].rearrange("c (b r) w -> c r b w", r=4)
     g_set = set(i for i in range(NOFF) if ((i + 1) * G_COUNT) // NOFF > (i * G_COUNT) // NOFF)
-    rest = [i for i in range(NOFF) if i not in g_set]
-    x_set = set(rest[j] for j in range(len(rest)) if ((j + 1) * X_COUNT) // len(rest) > (j * X_COUNT) // len(rest))
 
     with ExitStack() as ctx:
         const = ctx.enter_context(tc.tile_pool(name="const", bufs=1))
         work = ctx.enter_context(tc.tile_pool(name="work", bufs=2))
         affp = ctx.enter_context(tc.tile_pool(name="affp", bufs=2))
-        accp = ctx.enter_context(tc.tile_pool(name="accp", bufs=4))
-        ps_win = ctx.enter_context(tc.psum_pool(name="ps_win", bufs=5))
-        ps_aux = ctx.enter_context(tc.psum_pool(name="ps_aux", bufs=3))
+        ps_win = ctx.enter_context(tc.psum_pool(name="ps_win", bufs=2))
+        ps_pt = ctx.enter_context(tc.psum_pool(name="ps_pt", bufs=2))
+        ps_agg = ctx.enter_context(tc.psum_pool(name="ps_agg", bufs=2))
+        ps_aux = ctx.enter_context(tc.psum_pool(name="ps_aux", bufs=2))
 
+        pl = const.tile([P, PLW], BF16, name="pl")
+        nc.vector.memset(pl[:], 0.0)
+        one = const.tile([P, 1], F32, name="one")
+        nc.vector.memset(one[:], 1.0)
+        pk_a = const.tile([P, PKW], BF16, name="pk_a")
+        pk_b = const.tile([P, PKW], BF16, name="pk_b")
+        nc.vector.memset(pk_a[:], 0.0)
+        nc.vector.memset(pk_b[:], 0.0)
         x_raw = const.tile([P, 4, HW], BF16, name="x_raw")
         wf_raw = const.tile([P, 4, C], BF16, name="wf_raw")
         wu_raw = const.tile([P, 4, C], BF16, name="wu_raw")
-        chunks = [(0, 512), (512, 512), (1024, 512), (1536, 512), (2048, 256)]
-
-        pk_a = const.tile([P, PL], BF16, name="pk_a")
-        pk_b = const.tile([P, PL], BF16, name="pk_b")
-        one = const.tile([P, 1], F32, name="one")
-        nc.vector.memset(one[:], 1.0)
-        nc.vector.memset(pk_a[:], 0.0)
-        nc.gpsimd.memset(pk_b[:], 0.0)
         gam = const.tile([P, 4], BF16, name="gam")
         bet = const.tile([P, 4], BF16, name="bet")
         mea = const.tile([P, 4], BF16, name="mea")
@@ -69,37 +74,44 @@ def tile_dcblock_kernel(tc, x, coarse_probs, sigma, w_feat, w_fuse, bn_gamma, bn
         nc.scalar.dma_start(out=mea[:], in_=bn_mean.rearrange("(p j) -> p j", j=4))
         nc.scalar.dma_start(out=bet[:], in_=bn_beta.rearrange("(p j) -> p j", j=4))
         nc.scalar.dma_start(out=sig[:], in_=sigma.partition_broadcast(P))
-
         warm = const.tile([P, 1], F32, name="warm")
         nc.scalar.activation(out=warm[:], in_=one[:], func=ACT.Sqrt)
+
+        pl_rows = pl[:, PITCH:PITCH + 12 * PITCH].rearrange("p (b w) -> p b w", w=PITCH)
+        for rr in range(4):
+            nc.sync.dma_start(out=pl_rows[CP * rr:CP * rr + 16, :, 4:4 + IMG_W], in_=cp_r[0:16, rr])
+            nc.scalar.dma_start(out=pl_rows[CP * rr + 16:CP * rr + CP, :, 4:4 + IMG_W], in_=cp_r[16:CP, rr])
+        nc.sync.dma_start(out=x_raw[:, :, 0:768], in_=x_v[:, :, 0:768])
+        nc.sync.dma_start(out=wf_raw[:], in_=w_feat.rearrange("(m t) k -> m t k", t=4))
+        nc.sync.dma_start(out=x_raw[:, :, 1536:2304], in_=x_v[:, :, 1536:2304])
         for dix in range(KW):
             di = dix - 3
             pk = pk_a if dix < 4 else pk_b
             s = dix if dix < 4 else dix - 4
-            q_lo = max(0, PADP - IMG_W * di)
+            q_lo = max(PK0, PADP - IMG_W * di)
             q_hi = min(PL, HW + PADP - IMG_W * di)
             n_lo = q_lo - PADP + IMG_W * di
             n_hi = q_hi - PADP + IMG_W * di
-            nc.sync.dma_start(out=pk[CP * s:CP * s + 16, q_lo:q_hi], in_=cp_v[0:16, n_lo:n_hi])
-            nc.scalar.dma_start(out=pk[CP * s + 16:CP * s + CP, q_lo:q_hi], in_=cp_v[16:CP, n_lo:n_hi])
-
-        nc.sync.dma_start(out=x_raw[:, :, 0:512], in_=x_v[:, :, 0:512])
-        nc.sync.dma_start(out=wf_raw[:], in_=w_feat.rearrange("(m t) k -> m t k", t=4))
-        for c0, wd in chunks[1:]:
-            nc.sync.dma_start(out=x_raw[:, :, c0:c0 + wd], in_=x_v[:, :, c0:c0 + wd])
+            nc.sync.dma_start(out=pk[CP * s:CP * s + 16, q_lo - PK0:q_hi - PK0], in_=cp_v[0:16, n_lo:n_hi])
+            nc.scalar.dma_start(out=pk[CP * s + 16:CP * s + CP, q_lo - PK0:q_hi - PK0], in_=cp_v[16:CP, n_lo:n_hi])
+        nc.sync.dma_start(out=x_raw[:, :, 768:1536], in_=x_v[:, :, 768:1536])
         nc.sync.dma_start(out=wu_raw[:], in_=w_fuse.rearrange("(m t) k -> m t k", t=4))
 
-        ident_f = const.tile([P, P], F32, name="ident_f")
-        masks.make_identity(nc, ident_f[:])
         ident_b = const.tile([P, P], BF16, name="ident_b")
         masks.make_identity(nc, ident_b[:])
+        ident_f = const.tile([P, P], F32, name="ident_f")
+        masks.make_identity(nc, ident_f[:])
 
-        msg_e = const.tile([P, 4, ML], MSG_DT, name="msg_e")
-        msg_o = const.tile([P, 4, ML], MSG_DT, name="msg_o")
-        nc.gpsimd.memset(msg_e[:, :, 0:PADM], 0.0)
-        nc.gpsimd.memset(msg_e[:, :, PADM + HW:ML], 0.0)
-        nc.gpsimd.memset(msg_o[:, :, 0:PADM], 0.0)
-        nc.gpsimd.memset(msg_o[:, :, PADM + HW - 1:ML], 0.0)
+        bands = const.tile([P, 8, 4, 576], BF16, name="bands")
+        nc.gpsimd.memset(bands[:, :, :, 0:48], 0.0)
+        nc.gpsimd.memset(bands[:, 0, :, :], 0.0)
+        nc.gpsimd.memset(bands[:, 7, :, :], 0.0)
+        abig = work.tile([P, 3136], F32, name="abig", tag="big", align_bytes=64, bufs=1)
+        nc.gpsimd.memset(abig[:], 0.0)
+        msg_e = const.tile([P, 4, ML], BF16, name="msg_e")
+        msg_o = const.tile([P, 4, ML], BF16, name="msg_o")
+        nc.gpsimd.memset(msg_e[:, :, 760:ML], 0.0)
+        nc.gpsimd.memset(msg_o[:, :, 760:ML], 0.0)
 
         v1 = const.tile([P, 4], F32, name="v1")
         nc.vector.tensor_scalar_add(out=v1[:], in0=var[:], scalar1=1e-5)
@@ -127,9 +139,140 @@ def tile_dcblock_kernel(tc, x, coarse_probs, sigma, w_feat, w_fuse, bn_gamma, bn
         nc.vector.reciprocal(out=neginv[:], in_=sg[:])
         nc.vector.tensor_scalar_mul(out=neginv[:], in0=neginv[:], scalar1=-1.0)
 
-        NT = 2 * PAIRS
+        pz = const.tile([P, 10, 12, CP], BF16, name="pz")
+        for a in (-1, 0, 1):
+            for h in range(2):
+                pps = ps_pt.tile([P, 6, P], BF16, name="pps", tag="pt")
+                for j in range(6):
+                    s = PITCH * (1 + a) + 1 + 6 * h + j
+                    nc.tensor.transpose(pps[:, j, :], pl[:, s:s + 6 * (P - 1) + 1:6], ident_b[:])
+                rr0 = 1 if a == -1 else 0
+                rr1 = 3 if a == 1 else 4
+                ri0 = 4 * a + 3 + rr0
+                nc.vector.tensor_copy(
+                    out=pz[:, ri0:ri0 + rr1 - rr0, 6 * h:6 * h + 6, :].rearrange("p r j c -> p j r c"),
+                    in_=pps[:, :, 0:4 * CP].rearrange("p j (r c) -> p j r c", c=CP)[:, :, rr0:rr1, :],
+                )
+
+        def prep_weight(raw, label):
+            grouped = work.tile([P, 4 * C], BF16, name="grouped", tag="grouped", align_bytes=64, bufs=1)
+            gw = grouped[:].bitcast(F32).rearrange("p (t m u) -> p t m u", t=4, u=2)
+            for half in range(2):
+                ps = ps_aux.tile([P, 2, 2, P], F32, name=label + "_ps", tag="aux")
+                for tt in range(2):
+                    words = raw[:, 2 * half + tt, :].bitcast(F32)
+                    for u in range(2):
+                        nc.tensor.transpose(ps[:, tt, u, :], words[:, u::2], ident_f[:])
+                nc.vector.tensor_copy(out=gw[:, 2 * half:2 * half + 2], in_=ps[:].rearrange("p t u m -> p t m u"))
+            codes = const.tile([P, C], U32, name=label + "_codes", align_bytes=64)
+            scl = const.tile([P, C], U8, name=label + "_scl", align_bytes=64)
+            nc.vector.quantize_mx(out=codes[:].bitcast(FP8X4), scales=scl[:], in_=grouped[:])
+            return codes, scl
+
+        wf_codes, wf_scl = prep_weight(wf_raw, "wf")
+
+        x_codes = const.tile([P, HW], U32, name="x_codes", align_bytes=64)
+        x_scl = const.tile([P, HW], U8, name="x_scl", align_bytes=64)
+
+        def stage1_quant(g):
+            c0 = 768 * g
+            xn = work.tile([P, 4, 768], BF16, name="xn", tag="x2", align_bytes=64)
+            xg = work.tile([P, 768, 4], BF16, name="xg", tag="x2", align_bytes=64)
+            eng = nc.vector if g == 0 else nc.gpsimd
+            for j in range(4):
+                eng.tensor_scalar(
+                    out=xn[:, j, :], in0=x_raw[:, j, c0:c0 + 768],
+                    scalar1=bn_s[:, j:j + 1], scalar2=bn_b[:, j:j + 1], op0=ALU.mult, op1=ALU.add,
+                )
+            eng.tensor_copy(out=xg[:], in_=xn[:].rearrange("p j n -> p n j"))
+            for u in range(3):
+                n0 = c0 + 256 * u
+                nc.vector.quantize_mx(
+                    out=x_codes[:, n0:n0 + 256].bitcast(FP8X4), scales=x_scl[:, n0:n0 + 256],
+                    in_=xg[:, 256 * u:256 * u + 256, :].rearrange("p n j -> p (n j)"),
+                )
+
+        def stage1_mm(g):
+            c0 = 768 * g
+            nr = 16 if g < 2 else 12
+            b0 = 12 * (16 * g + 3)
+            for t in range(4):
+                bank = ps_aux.tile([P, 3, 256], BF16, name="bank", tag="aux")
+                for h in range(3):
+                    n0 = c0 + 256 * h
+                    nc.tensor.matmul_mx(
+                        out=bank[:, h, :],
+                        lhsT=wf_codes[:, P * t:P * t + P].bitcast(FP8X4), lhsT_scale=wf_scl[:, P * t:P * t + P],
+                        rhs=x_codes[:, n0:n0 + 256].bitcast(FP8X4), rhs_scale=x_scl[:, n0:n0 + 256],
+                        start=True, stop=True,
+                    )
+                flat = bank[:].rearrange("p h n -> p (h n)")
+                rows = flat.rearrange("p (r w) -> p r w", w=IMG_W)
+                dst = bands[:, :, t, b0:b0 + 12 * nr].rearrange("p b (r i) -> p b r i", i=12)
+                nc.scalar.copy(out=dst[:, 1:6:2], in_=rows[:, 0:nr, 3:39].rearrange("p r (b i) -> p b r i", i=12))
+                nc.scalar.copy(out=dst[:, 2:7:2], in_=rows[:, 0:nr, 9:45].rearrange("p r (b i) -> p b r i", i=12))
+                nc.scalar.copy(out=dst[:, 0, :, 3:12], in_=rows[:, 0:nr, 0:9])
+                nc.scalar.copy(out=dst[:, 7, :, 0:9], in_=rows[:, 0:nr, 39:48])
+                if g == 2:
+                    nc.scalar.copy(out=msg_e[:, t, 0:768], in_=flat)
+                    nc.scalar.copy(out=msg_o[:, t, 0:767], in_=flat[:, 1:768])
+
+        stage1_quant(0)
+        stage1_mm(0)
+
+        dist = const.tile([P, NPOS * NOFF], F32, name="dist")
+        zs_p = const.tile([P, NPOS], F32, name="zs_p")
+        rz_p = const.tile([P, NPOS], F32, name="rz_p")
+        a_sb = const.tile([P, 90, NPOS], F32, name="a_sb")
+
+        def a_group(g):
+            pdiff = affp.tile([P, 3, NOFF * CP], F32, name="pdiff", tag="diff")
+            for i in range(3):
+                ro, co = divmod(3 * g + i, 6)
+                nc.vector.tensor_tensor(
+                    out=pdiff[:, i, :].rearrange("p (d e c) -> p d e c", d=KW, c=CP),
+                    in0=pz[:, ro:ro + KW, co:co + KW, :],
+                    in1=pz[:, ro + 3:ro + 4, co + 3:co + 4, :].to_broadcast([P, KW, KW, CP]),
+                    op=ALU.subtract,
+                )
+            flat = pdiff[:].rearrange("p i f -> p (i f)")
+            nc.scalar.activation(out=flat, in_=flat, func=ACT.Square)
+            nc.vector.tensor_reduce(
+                out=dist[:, 3 * NOFF * g:3 * NOFF * (g + 1)],
+                in_=pdiff[:].rearrange("p i (f c) -> p (i f) c", c=CP), axis=AX.X, op=ALU.add,
+            )
+
+        def a_finish(ro):
+            d6 = dist[:, 6 * NOFF * ro:6 * NOFF * (ro + 1)]
+            nc.scalar.activation(out=d6, in_=d6, func=ACT.Exp, scale=neginv[:, 0:1])
+            nc.scalar.activation(out=d6, in_=d6, func=ACT.Exp, bias=-1.0)
+            nc.vector.tensor_reduce(
+                out=zs_p[:, 6 * ro:6 * ro + 6], in_=d6.rearrange("p (n f) -> p n f", f=NOFF), axis=AX.X, op=ALU.add,
+            )
+            nc.vector.reciprocal(out=rz_p[:, 6 * ro:6 * ro + 6], in_=zs_p[:, 6 * ro:6 * ro + 6])
+            s0 = ro * (6 * P + 12)
+            canvas = abig[:, s0:s0 + 6 * (P + 1)].rearrange("p (a x) -> p a x", x=P + 1)[:, :, 0:84]
+            nc.vector.tensor_tensor(
+                out=canvas.rearrange("p a (d e) -> p a d e", e=12)[:, :, :, 0:KW],
+                in0=d6.rearrange("p (a d e) -> p a d e", d=KW, e=KW),
+                in1=rz_p[:, 6 * ro:6 * ro + 6].unsqueeze(2).unsqueeze(3).to_broadcast([P, 6, KW, KW]),
+                op=ALU.mult,
+            )
+            for u in range(2):
+                n0 = 6 * ro + 3 * u
+                aps = ps_agg.tile([P, 3, P], F32, name="aps", tag="agg")
+                for j in range(3):
+                    nc.tensor.transpose(aps[:, j, :], abig[:, P * (n0 + j):P * (n0 + j) + P], ident_f[:])
+                nc.scalar.copy(out=a_sb[:, :, n0:n0 + 3], in_=aps[:, :, 0:90].rearrange("p j q -> p q j"))
+
+        for ro in range(4):
+            a_group(2 * ro)
+            a_group(2 * ro + 1)
+            a_finish(ro)
+
+        NT = 2 * len(E_PAIRS)
         n_i = const.tile([P, NT], I32, name="n_i")
-        nc.gpsimd.iota(n_i[:], pattern=[[2 * P, PAIRS], [1, 2]], base=0, channel_multiplier=2)
+        nc.gpsimd.iota(n_i[:], pattern=[[2 * P, len(E_PAIRS)], [1, 2]], base=PE_PIX, channel_multiplier=2)
         thr_i = const.tile([P, IMG_W - 1], I32, name="thr_i")
         nc.gpsimd.iota(thr_i[:], pattern=[[IMG_W, IMG_W - 1]], base=IMG_W, channel_multiplier=0)
         dj_i = const.tile([P, KW], I32, name="dj_i")
@@ -175,71 +318,13 @@ def tile_dcblock_kernel(tc, x, coarse_probs, sigma, w_feat, w_fuse, bn_gamma, bn
         mask49 = const.tile([P, NT, KW, KW], F32, name="mask49")
         nc.vector.tensor_copy(out=mask49[:], in_=mask7[:].unsqueeze(3).to_broadcast([P, NT, KW, KW]))
 
-        def prep_weight(raw, label):
-            grouped = const.tile([P, 4 * C], BF16, name=label + "_grouped", align_bytes=64)
-            gw = grouped[:].bitcast(F32).rearrange("p (t m u) -> p t m u", t=4, u=2)
-            for half in range(2):
-                ps = ps_aux.tile([P, 2, 2, P], F32, name=label + "_ps", tag="aux")
-                for tt in range(2):
-                    words = raw[:, 2 * half + tt, :].bitcast(F32)
-                    for u in range(2):
-                        nc.tensor.transpose(ps[:, tt, u, :], words[:, u::2], ident_f[:])
-                nc.vector.tensor_copy(out=gw[:, 2 * half:2 * half + 2], in_=ps[:].rearrange("p t u m -> p t m u"))
-            codes = const.tile([P, C], U32, name=label + "_codes", align_bytes=64)
-            scl = const.tile([P, C], U8, name=label + "_scl", align_bytes=64)
-            nc.vector.quantize_mx(out=codes[:].bitcast(FP8X4), scales=scl[:], in_=grouped[:])
-            return codes, scl
-
-        wf_codes, wf_scl = prep_weight(wf_raw, "wf")
-
-        x_codes = const.tile([P, HW], U32, name="x_codes", align_bytes=64)
-        x_scl = const.tile([P, HW], U8, name="x_scl", align_bytes=64)
-
-        def stage1(k):
-            c0, wd = chunks[k]
-            xn = work.tile([P, 4, wd], BF16, name="xn", tag="xn", bufs=1)
-            xg = work.tile([P, wd, 4], BF16, name="xg", tag="xg", align_bytes=64, bufs=1)
-            for j in range(4):
-                if k == 0:
-                    nc.vector.tensor_scalar(
-                        out=xn[:, j, :], in0=x_raw[:, j, c0:c0 + wd],
-                        scalar1=bn_s[:, j:j + 1], scalar2=bn_b[:, j:j + 1], op0=ALU.mult, op1=ALU.add,
-                    )
-                else:
-                    nc.scalar.activation(
-                        out=xn[:, j, :], in_=x_raw[:, j, c0:c0 + wd], func=ACT.Identity,
-                        scale=bn_s[:, j:j + 1], bias=bn_b[:, j:j + 1],
-                    )
-            if k == 0:
-                nc.vector.tensor_copy(out=xg[:], in_=xn[:].rearrange("p j n -> p n j"))
-            else:
-                nc.scalar.copy(out=xg[:], in_=xn[:].rearrange("p j n -> p n j"))
-            nc.vector.quantize_mx(
-                out=x_codes[:, c0:c0 + wd].bitcast(FP8X4), scales=x_scl[:, c0:c0 + wd],
-                in_=xg[:].rearrange("p n j -> p (n j)"),
-            )
-            for i in range(4 if wd == 512 else 2):
-                bank = ps_win.tile([P, 2, 256], MSG_DT, name="bank", tag="win")
-                for h in range(2):
-                    t = i if wd == 512 else 2 * i + h
-                    n0 = c0 + 256 * h if wd == 512 else c0
-                    nc.tensor.matmul_mx(
-                        out=bank[:, h, :],
-                        lhsT=wf_codes[:, P * t:P * t + P].bitcast(FP8X4), lhsT_scale=wf_scl[:, P * t:P * t + P],
-                        rhs=x_codes[:, n0:n0 + 256].bitcast(FP8X4), rhs_scale=x_scl[:, n0:n0 + 256],
-                        start=True, stop=True,
-                    )
-                if wd == 512:
-                    nc.scalar.copy(out=msg_e[:, i, PADM + c0:PADM + c0 + 512], in_=bank[:].rearrange("p h n -> p (h n)"))
-                    nc.scalar.copy(out=msg_o[:, i, PADM + c0 - 1:PADM + c0 + 511], in_=bank[:].rearrange("p h n -> p (h n)"))
-                else:
-                    nc.scalar.copy(out=msg_e[:, 2 * i:2 * i + 2, PADM + c0:PADM + c0 + 256], in_=bank[:])
-                    nc.scalar.copy(out=msg_o[:, 2 * i:2 * i + 2, PADM + c0 - 1:PADM + c0 + 255], in_=bank[:])
+        later = {}
 
         def affinity(pi):
+            pp = pi - E_PAIRS[0]
             diff = affp.tile([P, 2, NOFF + 1, CP], F32, name="diff", tag="diff")
             for a in range(2):
-                n0 = PADP + 2 * P * pi + a - 3
+                n0 = PADP + 2 * P * pi + a - 3 - PK0
                 win_a = ps_aux.tile([P, KW, P], BF16, name="win_a", tag="aux")
                 win_b = ps_aux.tile([P, KW, P], BF16, name="win_b", tag="aux")
                 for djx in range(KW):
@@ -259,16 +344,16 @@ def tile_dcblock_kernel(tc, x, coarse_probs, sigma, w_feat, w_fuse, bn_gamma, bn
                 )
             flat = diff[:].rearrange("p a f c -> p (a f c)")
             nc.scalar.activation(out=flat, in_=flat, func=ACT.Square)
-            dist = affp.tile([P, 2 * (NOFF + 1)], F32, name="dist", tag="dist")
-            nc.vector.tensor_reduce(out=dist[:], in_=diff[:].rearrange("p a f c -> p (a f) c"), axis=AX.X, op=ALU.add)
+            dst = affp.tile([P, 2 * (NOFF + 1)], F32, name="dst", tag="dst")
+            nc.vector.tensor_reduce(out=dst[:], in_=diff[:].rearrange("p a f c -> p (a f) c"), axis=AX.X, op=ALU.add)
             gau = affp.tile([P, 2 * (NOFF + 1)], F32, name="gau", tag="gau")
-            nc.scalar.activation(out=gau[:], in_=dist[:], func=ACT.Exp, scale=neginv[:, 0:1])
+            nc.scalar.activation(out=gau[:], in_=dst[:], func=ACT.Exp, scale=neginv[:, 0:1])
             ex = affp.tile([P, 2, NOFF + 1], F32, name="ex", tag="ex")
             nc.scalar.activation(out=ex[:].rearrange("p a f -> p (a f)"), in_=gau[:], func=ACT.Exp, bias=-1.0)
             em = affp.tile([P, 2, NOFF], F32, name="em", tag="em")
             nc.gpsimd.tensor_tensor(
                 out=em[:], in0=ex[:, :, 0:NOFF],
-                in1=mask49[:, 2 * pi:2 * pi + 2].rearrange("p t j i -> p t (j i)"), op=ALU.mult,
+                in1=mask49[:, 2 * pp:2 * pp + 2].rearrange("p t j i -> p t (j i)"), op=ALU.mult,
             )
             zs = affp.tile([P, 2], F32, name="zs", tag="zs")
             nc.vector.tensor_reduce(out=zs[:], in_=em[:], axis=AX.X, op=ALU.add)
@@ -276,85 +361,20 @@ def tile_dcblock_kernel(tc, x, coarse_probs, sigma, w_feat, w_fuse, bn_gamma, bn
             for a in range(2):
                 nc.scalar.activation(
                     out=zo[:, a:a + 1], in_=ex[:, a, NOFF:NOFF + 1], func=ACT.Identity,
-                    scale=cnt[:, 2 * pi + a:2 * pi + a + 1], bias=zs[:, a:a + 1],
+                    scale=cnt[:, 2 * pp + a:2 * pp + a + 1], bias=zs[:, a:a + 1],
                 )
             rz = affp.tile([P, 2], F32, name="rz", tag="rz")
             nc.vector.reciprocal(out=rz[:], in_=zo[:])
-            wa = affp.tile([P, 2, NOFF], F32, name="wa", tag="wa", bufs=3)
+            wa = affp.tile([P, 2, NOFF], F32, name="wa", tag="wa")
             for a in range(2):
                 nc.scalar.activation(out=wa[:, a, :], in_=em[:, a, :], func=ACT.Copy, scale=rz[:, a:a + 1])
-            return wa
+            later[("wa", pi)] = wa
 
-        def aggregate(pi, wa, hooks):
-            acc_v = accp.tile([P, 2, C], F32, name="acc_v", tag="acc_v", bufs=3)
-            acc_g0 = accp.tile([P, 2, C], F32, name="acc_g0", tag="acc_g")
-            acc_g1 = accp.tile([P, 2, C], F32, name="acc_g1", tag="acc_g")
-            acc_g = [acc_g0, acc_g1]
-            parts = []
-            seen_v = 0
-            seen_g = 0
-            for f in range(NOFF):
-                for hook in hooks.get(f, []):
-                    hook()
-                djx, dix = divmod(f, KW)
-                shift = IMG_W * (dix - 3) + (djx - 3)
-                if f in x_set:
-                    prod = accp.tile([P, 2, C], F32, name="xprod", tag="xprod", bufs=X_COUNT + 3)
-                    parts.append(prod)
-                if f in g_set:
-                    if seen_g < 2:
-                        prod = acc_g[seen_g]
-                    else:
-                        prod = accp.tile([P, 2, C], F32, name="prod", tag="prod", bufs=3)
-                base = PADM + 2 * P * pi + shift
-                src = msg_e if base % 2 == 0 else msg_o
-                word0 = base // 2
-                win = ps_win.tile([P, C], F32, name="win", tag="win")
-                for t in range(4):
-                    nc.tensor.transpose(win[:, P * t:P * t + P], src[:, t, :].bitcast(F32)[:, word0:word0 + P], ident_f[:])
-                halves = win[:].bitcast(BF16)
-                for a in range(2):
-                    wcol = wa[:, a, f:f + 1]
-                    if f in g_set or f in x_set:
-                        nc.scalar.activation(out=prod[:, a, :], in_=halves[:, a::2], func=ACT.Copy, scale=wcol)
-                    elif seen_v == 0:
-                        nc.vector.tensor_scalar(out=acc_v[:, a, :], in0=halves[:, a::2], scalar1=wcol, scalar2=None, op0=ALU.mult)
-                    else:
-                        nc.vector.scalar_tensor_tensor(
-                            out=acc_v[:, a, :], in0=halves[:, a::2], scalar=wcol, in1=acc_v[:, a, :], op0=ALU.mult, op1=ALU.add,
-                        )
-                if f in g_set:
-                    if seen_g >= 2:
-                        tgt = acc_g[seen_g % 2]
-                        nc.gpsimd.tensor_tensor(out=tgt[:], in0=tgt[:], in1=prod[:], op=ALU.add)
-                    seen_g += 1
-                elif f not in x_set:
-                    seen_v += 1
-            return parts + [acc_g0, acc_g1, acc_v]
-
-        def turn_back(parts, held, a, t):
-            if a == 0 and t == 0:
-                held["ag"] = work.tile([P, 2 * P, 4], BF16, name="ag", tag="ag", align_bytes=64)
-            if t == 0:
-                held["back"] = ps_aux.tile([P, 4, P], F32, name="back", tag="aux")
-            back = held["back"]
-            for i in range(len(parts)):
-                nc.tensor.matmul(
-                    out=back[:, t, :], lhsT=parts[i][:, a, P * t:P * t + P], rhs=ident_f[:],
-                    is_transpose=True, start=(i == 0), stop=(i == len(parts) - 1),
-                )
-            if t == 3:
-                nc.scalar.copy(
-                    out=held["ag"][:].rearrange("p (n a) t -> p a n t", a=2)[:, a], in_=back[:].rearrange("p t n -> p n t"),
-                )
-
-        def stage2(pi, held):
-            ag = held["ag"]
+        def stage2(n0, ag_flat):
             a_codes = work.tile([P, 2 * P], U32, name="a_codes", tag="a_codes", align_bytes=64)
             a_scl = work.tile([P, 2 * P], U8, name="a_scl", tag="a_scl", align_bytes=64)
-            nc.vector.quantize_mx(out=a_codes[:].bitcast(FP8X4), scales=a_scl[:], in_=ag[:].rearrange("p n t -> p (n t)"))
+            nc.vector.quantize_mx(out=a_codes[:].bitcast(FP8X4), scales=a_scl[:], in_=ag_flat)
             o_sb = work.tile([P, 4, 2 * P], F32, name="o_sb", tag="o_sb")
-            n0 = 2 * P * pi
             for u in range(2):
                 ps2 = ps_aux.tile([P, 2, 2 * P], F32, name="ps2", tag="aux")
                 for h in range(2):
@@ -370,34 +390,137 @@ def tile_dcblock_kernel(tc, x, coarse_probs, sigma, w_feat, w_fuse, bn_gamma, bn
                 )
             nc.sync.dma_start(out=out_v[:, :, n0:n0 + 2 * P], in_=o_sb[:])
 
-        later = {}
+        def e_begin(pi):
+            later[("acc", pi)] = work.tile([P, 2, C], F32, name="acc_v", tag="acc_v")
+            later[("acg", pi)] = work.tile([P, 2, C], F32, name="acc_g", tag="acc_g")
 
-        def make_weights():
-            later["wu"] = prep_weight(wu_raw, "wu")
+        def e_step(pi, f):
+            acc = later[("acc", pi)]
+            wa = later[("wa", pi)]
+            djx, dix = divmod(f, KW)
+            base = 2 * P * pi - ME0 + IMG_W * (dix - 3) + (djx - 3)
+            src = msg_e if base % 2 == 0 else msg_o
+            word0 = base // 2
+            win = ps_win.tile([P, C], F32, name="win", tag="win")
+            for t in range(4):
+                nc.tensor.transpose(win[:, P * t:P * t + P], src[:, t, :].bitcast(F32)[:, word0:word0 + P], ident_f[:])
+            halves = win[:].bitcast(BF16)
+            acg = later[("acg", pi)]
+            first_g = f == min(g_set)
+            first_v = f == min(i for i in range(NOFF) if i not in g_set)
+            if f in g_set:
+                prod = acg if first_g else work.tile([P, 2, C], F32, name="prod", tag="prod")
+            for a in range(2):
+                wcol = wa[:, a, f:f + 1]
+                if f in g_set:
+                    nc.scalar.activation(out=prod[:, a, :], in_=halves[:, a::2], func=ACT.Copy, scale=wcol)
+                elif first_v:
+                    nc.vector.tensor_scalar(out=acc[:, a, :], in0=halves[:, a::2], scalar1=wcol, scalar2=None, op0=ALU.mult)
+                else:
+                    nc.vector.scalar_tensor_tensor(
+                        out=acc[:, a, :], in0=halves[:, a::2], scalar=wcol, in1=acc[:, a, :], op0=ALU.mult, op1=ALU.add,
+                    )
+            if f in g_set and not first_g:
+                nc.gpsimd.tensor_tensor(out=acg[:], in0=acg[:], in1=prod[:], op=ALU.add)
+            if f == NOFF - 1:
+                nc.gpsimd.tensor_tensor(out=acg[:], in0=acg[:], in1=acc[:], op=ALU.add)
 
-        def make_affinity(pi):
-            later["wa"] = affinity(pi)
+        def turn_back(pi, a):
+            acc = later[("acg", pi)]
+            if a == 0:
+                later[("ag", pi)] = work.tile([P, 2 * P, 4], BF16, name="ag", tag="ag", align_bytes=64)
+            back = ps_aux.tile([P, 4, P], F32, name="back", tag="aux")
+            for t in range(4):
+                nc.tensor.transpose(back[:, t, :], acc[:, a, P * t:P * t + P], ident_f[:])
+            nc.scalar.copy(
+                out=later[("ag", pi)][:].rearrange("p (n a) t -> p a n t", a=2)[:, a], in_=back[:].rearrange("p t n -> p n t"),
+            )
 
-        stage1(0)
-        make_affinity(0)
-        before = None
-        for pi in range(PAIRS):
-            wa_now = later["wa"]
-            hooks = {}
-            if pi == 0:
-                hooks[4] = [lambda: stage1(1)]
-                hooks[10] = [make_weights]
-            if pi in (1, 3, 5):
-                hooks[18] = [lambda k=(pi + 3) // 2: stage1(k)]
-            if before is not None:
-                held = {}
-                for i in range(8):
-                    hooks[2 * i + 1] = [lambda pp=before, hh=held, a=i // 4, t=i % 4: turn_back(pp, hh, a, t)]
-                hooks[17] = [lambda q=pi - 1, hh=held: stage2(q, hh)]
-            if pi + 1 < PAIRS:
-                hooks[20] = [lambda q=pi + 1: make_affinity(q)]
-            before = aggregate(pi, wa_now, hooks)
-        held = {}
-        for i in range(8):
-            turn_back(before, held, i // 4, i % 4)
-        stage2(PAIRS - 1, held)
+        def e_stage2(pi):
+            stage2(2 * P * pi, later[("ag", pi)][:].rearrange("p n t -> p (n t)"))
+
+        ag_all = work.tile([P, 1920, 4], BF16, name="ag_all", tag="big", align_bytes=64, bufs=1)
+        plist = [(rb, cb) for rb in range(10) for cb in range(8)]
+
+        def p_front(idx):
+            rb, cb = plist[idx]
+            pt = ps_pt.tile([P, 4, P], BF16, name="pt", tag="pt")
+            for t in range(4):
+                nc.tensor.transpose(pt[:, t, :], bands[:, cb, t, 48 * rb:48 * rb + P], ident_b[:])
+            pf = work.tile([P, 4, P], F32, name="pf", tag="pf", bufs=4)
+            nc.scalar.copy(out=pf[:], in_=pt[:])
+            later[("pf", idx)] = pf
+
+        def p_back(idx):
+            rb, cb = plist[idx]
+            half, cc = divmod(cb, 4)
+            if cc == 0:
+                later["aggps"] = ps_agg.tile([P, 4, 4, NPOS], F32, name="aggps", tag="agg")
+            aggps = later["aggps"]
+            pf = later[("pf", idx)]
+            nro = 4 if rb < 9 else (2 if cb < 3 else 1)
+            for t in range(4):
+                nc.tensor.matmul(
+                    out=aggps[:, t, 0:nro, 6 * cc:6 * cc + 6], lhsT=pf[:, t, :],
+                    rhs=a_sb[:, 9 * rb + cb, 0:6 * nro].rearrange("p (r c) -> p r c", c=6),
+                    start=True, stop=True,
+                )
+            if cc == 3:
+                dst = ag_all[:, 192 * rb:192 * rb + 192, :].rearrange("p (r w) t -> p r w t", w=IMG_W)
+                if rb < 9:
+                    pieces = [(0, 4, 24)]
+                elif half == 0:
+                    pieces = [(0, 1, 24), (1, 2, 16)]
+                else:
+                    pieces = [(0, 1, 24)]
+                for ra, rz_, ncol in pieces:
+                    nc.scalar.copy(
+                        out=dst[:, ra:rz_, 24 * half:24 * half + ncol, :],
+                        in_=aggps[:, :, ra:rz_, 0:ncol].rearrange("p t r c -> p r c t"),
+                    )
+                if half == 1:
+                    ready = min(192 * (rb + 1), PE_PIX)
+                    while 256 * (later["chunk"] + 1) <= ready:
+                        n0 = 256 * later["chunk"]
+                        stage2(n0, ag_all[:, n0:n0 + 256, :].rearrange("p n t -> p (n t)"))
+                        later["chunk"] = later["chunk"] + 1
+
+        stage1_quant(2)
+        stage1_mm(2)
+        later["wu"] = prep_weight(wu_raw, "wu")
+        affinity(E_PAIRS[0])
+        stage1_quant(1)
+        stage1_mm(1)
+        later["chunk"] = 0
+
+        e_items = []
+        first, second = E_PAIRS
+        e_items.append(lambda: e_begin(first))
+        for f in range(NOFF):
+            e_items.append(lambda f=f: e_step(first, f))
+            if f == 20:
+                e_items.append(lambda: affinity(second))
+        e_items.append(lambda: e_begin(second))
+        for f in range(NOFF):
+            e_items.append(lambda f=f: e_step(second, f))
+            if f == 1:
+                e_items.append(lambda: turn_back(first, 0))
+            if f == 3:
+                e_items.append(lambda: turn_back(first, 1))
+            if f == 6:
+                e_items.append(lambda: e_stage2(first))
+        e_items.append(lambda: turn_back(second, 0))
+        e_items.append(lambda: turn_back(second, 1))
+        e_items.append(lambda: e_stage2(second))
+
+        n_e = len(e_items)
+        done_e = 0
+        for ip in range(len(plist) + 2):
+            if ip < len(plist):
+                p_front(ip)
+            if ip >= 2:
+                p_back(ip - 2)
+            want = min(n_e, ((ip + 1) * n_e) // E_SPAN)
+            while done_e < want:
+                e_items[done_e]()
+                done_e += 1

@@ -33,6 +33,7 @@ PLW = 918
 NPOS = 24
 E_SPAN = 68
 G_COUNT = 16
+HEAD_STEPS = 30
 FLOPS = 2 * 2 * C * C * HW + 2 * NOFF * C * HW + 3 * NOFF * CP * HW
 
 
@@ -107,11 +108,11 @@ def tile_dcblock_kernel(tc, x, coarse_probs, sigma, w_feat, w_fuse, bn_gamma, bn
         nc.gpsimd.memset(bands[:, 0, :, :], 0.0)
         nc.gpsimd.memset(bands[:, 7, :, :], 0.0)
         abig = work.tile([P, 3136], F32, name="abig", tag="big", align_bytes=64, bufs=1)
-        nc.gpsimd.memset(abig[:], 0.0)
+        nc.vector.memset(abig[:], 0.0)
         msg_e = const.tile([P, 4, ML], BF16, name="msg_e")
         msg_o = const.tile([P, 4, ML], BF16, name="msg_o")
-        nc.gpsimd.memset(msg_e[:, :, 760:ML], 0.0)
-        nc.gpsimd.memset(msg_o[:, :, 760:ML], 0.0)
+        nc.vector.memset(msg_e[:, :, 760:ML], 0.0)
+        nc.vector.memset(msg_o[:, :, 760:ML], 0.0)
 
         v1 = const.tile([P, 4], F32, name="v1")
         nc.vector.tensor_scalar_add(out=v1[:], in0=var[:], scalar1=1e-5)
@@ -178,7 +179,7 @@ def tile_dcblock_kernel(tc, x, coarse_probs, sigma, w_feat, w_fuse, bn_gamma, bn
             c0 = 768 * g
             xn = work.tile([P, 4, 768], BF16, name="xn", tag="x2", align_bytes=64)
             xg = work.tile([P, 768, 4], BF16, name="xg", tag="x2", align_bytes=64)
-            eng = nc.vector if g == 0 else nc.gpsimd
+            eng = nc.vector
             for j in range(4):
                 eng.tensor_scalar(
                     out=xn[:, j, :], in0=x_raw[:, j, c0:c0 + 768],
@@ -229,7 +230,7 @@ def tile_dcblock_kernel(tc, x, coarse_probs, sigma, w_feat, w_fuse, bn_gamma, bn
             pdiff = affp.tile([P, 3, NOFF * CP], F32, name="pdiff", tag="diff")
             for i in range(3):
                 ro, co = divmod(3 * g + i, 6)
-                nc.vector.tensor_tensor(
+                nc.gpsimd.tensor_tensor(
                     out=pdiff[:, i, :].rearrange("p (d e c) -> p d e c", d=KW, c=CP),
                     in0=pz[:, ro:ro + KW, co:co + KW, :],
                     in1=pz[:, ro + 3:ro + 4, co + 3:co + 4, :].to_broadcast([P, KW, KW, CP]),
@@ -264,11 +265,6 @@ def tile_dcblock_kernel(tc, x, coarse_probs, sigma, w_feat, w_fuse, bn_gamma, bn
                 for j in range(3):
                     nc.tensor.transpose(aps[:, j, :], abig[:, P * (n0 + j):P * (n0 + j) + P], ident_f[:])
                 nc.scalar.copy(out=a_sb[:, :, n0:n0 + 3], in_=aps[:, :, 0:90].rearrange("p j q -> p q j"))
-
-        for ro in range(4):
-            a_group(2 * ro)
-            a_group(2 * ro + 1)
-            a_finish(ro)
 
         NT = 2 * len(E_PAIRS)
         n_i = const.tile([P, NT], I32, name="n_i")
@@ -406,13 +402,14 @@ def tile_dcblock_kernel(tc, x, coarse_probs, sigma, w_feat, w_fuse, bn_gamma, bn
                 nc.tensor.transpose(win[:, P * t:P * t + P], src[:, t, :].bitcast(F32)[:, word0:word0 + P], ident_f[:])
             halves = win[:].bitcast(BF16)
             acg = later[("acg", pi)]
-            first_g = f == min(g_set)
-            first_v = f == min(i for i in range(NOFF) if i not in g_set)
-            if f in g_set:
+            on_g = [i for i in range(NOFF) if i in g_set and not (pi == E_PAIRS[0] and i < HEAD_STEPS)]
+            first_g = f == min(on_g)
+            first_v = f == min(i for i in range(NOFF) if i not in on_g)
+            if f in on_g:
                 prod = acg if first_g else work.tile([P, 2, C], F32, name="prod", tag="prod")
             for a in range(2):
                 wcol = wa[:, a, f:f + 1]
-                if f in g_set:
+                if f in on_g:
                     nc.scalar.activation(out=prod[:, a, :], in_=halves[:, a::2], func=ACT.Copy, scale=wcol)
                 elif first_v:
                     nc.vector.tensor_scalar(out=acc[:, a, :], in0=halves[:, a::2], scalar1=wcol, scalar2=None, op0=ALU.mult)
@@ -420,7 +417,7 @@ def tile_dcblock_kernel(tc, x, coarse_probs, sigma, w_feat, w_fuse, bn_gamma, bn
                     nc.vector.scalar_tensor_tensor(
                         out=acc[:, a, :], in0=halves[:, a::2], scalar=wcol, in1=acc[:, a, :], op0=ALU.mult, op1=ALU.add,
                     )
-            if f in g_set and not first_g:
+            if f in on_g and not first_g:
                 nc.gpsimd.tensor_tensor(out=acg[:], in0=acg[:], in1=prod[:], op=ALU.add)
             if f == NOFF - 1:
                 nc.gpsimd.tensor_tensor(out=acg[:], in0=acg[:], in1=acc[:], op=ALU.add)
@@ -439,7 +436,6 @@ def tile_dcblock_kernel(tc, x, coarse_probs, sigma, w_feat, w_fuse, bn_gamma, bn
         def e_stage2(pi):
             stage2(2 * P * pi, later[("ag", pi)][:].rearrange("p n t -> p (n t)"))
 
-        ag_all = work.tile([P, 1920, 4], BF16, name="ag_all", tag="big", align_bytes=64, bufs=1)
         plist = [(rb, cb) for rb in range(10) for cb in range(8)]
 
         def p_front(idx):
@@ -485,20 +481,32 @@ def tile_dcblock_kernel(tc, x, coarse_probs, sigma, w_feat, w_fuse, bn_gamma, bn
                         stage2(n0, ag_all[:, n0:n0 + 256, :].rearrange("p n t -> p (n t)"))
                         later["chunk"] = later["chunk"] + 1
 
+        first, second = E_PAIRS
         stage1_quant(2)
+        a_group(0)
         stage1_mm(2)
-        later["wu"] = prep_weight(wu_raw, "wu")
-        affinity(E_PAIRS[0])
-        stage1_quant(1)
-        stage1_mm(1)
+        affinity(first)
+        e_begin(first)
+        for g in range(8):
+            if g > 0:
+                a_group(g)
+            if g % 2 == 1:
+                a_finish(g // 2)
+            for f in range((g * HEAD_STEPS) // 8, ((g + 1) * HEAD_STEPS) // 8):
+                e_step(first, f)
+            if g == 2:
+                stage1_quant(1)
+            if g == 3:
+                stage1_mm(1)
+            if g == 5:
+                later["wu"] = prep_weight(wu_raw, "wu")
+        ag_all = work.tile([P, 1920, 4], BF16, name="ag_all", tag="big", align_bytes=64, bufs=1)
         later["chunk"] = 0
 
         e_items = []
-        first, second = E_PAIRS
-        e_items.append(lambda: e_begin(first))
-        for f in range(NOFF):
+        for f in range(HEAD_STEPS, NOFF):
             e_items.append(lambda f=f: e_step(first, f))
-            if f == 20:
+            if f == HEAD_STEPS + 4:
                 e_items.append(lambda: affinity(second))
         e_items.append(lambda: e_begin(second))
         for f in range(NOFF):

@@ -31,7 +31,7 @@ PKW = 528
 PITCH = 54
 PLW = 918
 NPOS = 24
-E_SPAN = 68
+E_SPAN = 64
 G_COUNT = 16
 HEAD_STEPS = 30
 FLOPS = 2 * 2 * C * C * HW + 2 * NOFF * C * HW + 3 * NOFF * CP * HW
@@ -63,8 +63,7 @@ def tile_dcblock_kernel(tc, x, coarse_probs, sigma, w_feat, w_fuse, bn_gamma, bn
         nc.vector.memset(pk_a[:], 0.0)
         nc.vector.memset(pk_b[:], 0.0)
         x_raw = const.tile([P, 4, HW], BF16, name="x_raw")
-        wf_raw = const.tile([P, 4, C], BF16, name="wf_raw")
-        wu_raw = const.tile([P, 4, C], BF16, name="wu_raw")
+        wf_raw = work.tile([P, 4, C], BF16, name="wf_raw", tag="w_raw", bufs=1)
         gam = const.tile([P, 4], BF16, name="gam")
         bet = const.tile([P, 4], BF16, name="bet")
         mea = const.tile([P, 4], BF16, name="mea")
@@ -96,7 +95,6 @@ def tile_dcblock_kernel(tc, x, coarse_probs, sigma, w_feat, w_fuse, bn_gamma, bn
             nc.sync.dma_start(out=pk[CP * s:CP * s + 16, q_lo - PK0:q_hi - PK0], in_=cp_v[0:16, n_lo:n_hi])
             nc.scalar.dma_start(out=pk[CP * s + 16:CP * s + CP, q_lo - PK0:q_hi - PK0], in_=cp_v[16:CP, n_lo:n_hi])
         nc.sync.dma_start(out=x_raw[:, :, 768:1536], in_=x_v[:, :, 768:1536])
-        nc.sync.dma_start(out=wu_raw[:], in_=w_fuse.rearrange("(m t) k -> m t k", t=4))
 
         ident_b = const.tile([P, P], BF16, name="ident_b")
         masks.make_identity(nc, ident_b[:])
@@ -147,9 +145,9 @@ def tile_dcblock_kernel(tc, x, coarse_probs, sigma, w_feat, w_fuse, bn_gamma, bn
                 for j in range(6):
                     s = PITCH * (1 + a) + 1 + 6 * h + j
                     nc.tensor.transpose(pps[:, j, :], pl[:, s:s + 6 * (P - 1) + 1:6], ident_b[:])
-                rr0 = 1 if a == -1 else 0
-                rr1 = 3 if a == 1 else 4
-                ri0 = 4 * a + 3 + rr0
+                rr0 = 0
+                rr1 = 2 if a == 1 else 4
+                ri0 = 4 * a + 4
                 nc.vector.tensor_copy(
                     out=pz[:, ri0:ri0 + rr1 - rr0, 6 * h:6 * h + 6, :].rearrange("p r j c -> p j r c"),
                     in_=pps[:, :, 0:4 * CP].rearrange("p j (r c) -> p j r c", c=CP)[:, :, rr0:rr1, :],
@@ -171,6 +169,8 @@ def tile_dcblock_kernel(tc, x, coarse_probs, sigma, w_feat, w_fuse, bn_gamma, bn
             return codes, scl
 
         wf_codes, wf_scl = prep_weight(wf_raw, "wf")
+        wu_raw = work.tile([P, 4, C], BF16, name="wu_raw", tag="w_raw", bufs=1)
+        nc.sync.dma_start(out=wu_raw[:], in_=w_fuse.rearrange("(m t) k -> m t k", t=4))
 
         x_codes = const.tile([P, HW], U32, name="x_codes", align_bytes=64)
         x_scl = const.tile([P, HW], U8, name="x_scl", align_bytes=64)
@@ -225,6 +225,9 @@ def tile_dcblock_kernel(tc, x, coarse_probs, sigma, w_feat, w_fuse, bn_gamma, bn
         zs_p = const.tile([P, NPOS], F32, name="zs_p")
         rz_p = const.tile([P, NPOS], F32, name="rz_p")
         a_sb = const.tile([P, 90, NPOS], F32, name="a_sb")
+        a_top = const.tile([P, 8, 42], F32, name="a_top")
+        atop = const.tile([P, 18 * P + 64], F32, name="atop")
+        nc.vector.memset(atop[:], 0.0)
 
         def a_group(g):
             pdiff = affp.tile([P, 3, NOFF * CP], F32, name="pdiff", tag="diff")
@@ -265,6 +268,25 @@ def tile_dcblock_kernel(tc, x, coarse_probs, sigma, w_feat, w_fuse, bn_gamma, bn
                 for j in range(3):
                     nc.tensor.transpose(aps[:, j, :], abig[:, P * (n0 + j):P * (n0 + j) + P], ident_f[:])
                 nc.scalar.copy(out=a_sb[:, :, n0:n0 + 3], in_=aps[:, :, 0:90].rearrange("p j q -> p q j"))
+            if ro == 0:
+                return
+            nd = ro + 3
+            t0 = (ro - 1) * 6 * P
+            canvas = atop[:, t0:t0 + 6 * (P + 1)].rearrange("p (a x) -> p a x", x=P + 1)[:, :, 0:12 * nd]
+            nc.vector.tensor_tensor(
+                out=canvas.rearrange("p a (d e) -> p a d e", e=12)[:, :, :, 0:KW],
+                in0=d6.rearrange("p (a d e) -> p a d e", d=KW, e=KW)[:, :, KW - nd:KW, :],
+                in1=rz_p[:, 6 * ro:6 * ro + 6].unsqueeze(2).unsqueeze(3).to_broadcast([P, 6, nd, KW]),
+                op=ALU.mult,
+            )
+            for u in range(2):
+                n0 = 6 * (ro - 1) + 3 * u
+                aps = ps_agg.tile([P, 3, P], F32, name="aps", tag="agg")
+                for j in range(3):
+                    nc.tensor.transpose(aps[:, j, :], atop[:, P * (n0 + j):P * (n0 + j) + P], ident_f[:])
+                nc.scalar.copy(out=a_top[:, :, n0:n0 + 3], in_=aps[:, :, 0:8].rearrange("p j q -> p q j"))
+            if ro == 3:
+                nc.scalar.copy(out=a_top[:, :, 18:42], in_=a_sb[:, 9:17, :])
 
         NT = 2 * len(E_PAIRS)
         n_i = const.tile([P, NT], I32, name="n_i")
@@ -436,46 +458,61 @@ def tile_dcblock_kernel(tc, x, coarse_probs, sigma, w_feat, w_fuse, bn_gamma, bn
         def e_stage2(pi):
             stage2(2 * P * pi, later[("ag", pi)][:].rearrange("p n t -> p (n t)"))
 
-        plist = [(rb, cb) for rb in range(10) for cb in range(8)]
+        plist = [(c, cb) for c in range(1, 10) for cb in range(8)]
 
         def p_front(idx):
-            rb, cb = plist[idx]
+            c, cb = plist[idx]
             pt = ps_pt.tile([P, 4, P], BF16, name="pt", tag="pt")
             for t in range(4):
-                nc.tensor.transpose(pt[:, t, :], bands[:, cb, t, 48 * rb:48 * rb + P], ident_b[:])
-            pf = work.tile([P, 4, P], F32, name="pf", tag="pf", bufs=4)
+                nc.tensor.transpose(pt[:, t, :], bands[:, cb, t, 48 * c - 12:48 * c - 12 + P], ident_b[:])
+            pf = work.tile([P, 4, P], F32, name="pf", tag="pf", bufs=3)
             nc.scalar.copy(out=pf[:], in_=pt[:])
             later[("pf", idx)] = pf
 
         def p_back(idx):
-            rb, cb = plist[idx]
+            c, cb = plist[idx]
             half, cc = divmod(cb, 4)
-            if cc == 0:
-                later["aggps"] = ps_agg.tile([P, 4, 4, NPOS], F32, name="aggps", tag="agg")
-            aggps = later["aggps"]
             pf = later[("pf", idx)]
-            nro = 4 if rb < 9 else (2 if cb < 3 else 1)
+            if c == 1:
+                nro = 7
+                rhs = a_top[:, cb, :]
+                if cc == 0:
+                    for u in range(2):
+                        later[("aggps", u)] = ps_agg.tile([P, 2, 7, NPOS], F32, name="aggtop", tag="agg")
+            else:
+                nro = 4 if c < 9 else (3 if cb < 3 else 2)
+                rhs = a_sb[:, 9 * c + cb, 0:6 * nro]
+                if cc == 0:
+                    later[("aggps", 0)] = ps_agg.tile([P, 4, 4, NPOS], F32, name="aggps", tag="agg")
             for t in range(4):
+                spot = later[("aggps", t // 2)][:, t % 2] if c == 1 else later[("aggps", 0)][:, t]
                 nc.tensor.matmul(
-                    out=aggps[:, t, 0:nro, 6 * cc:6 * cc + 6], lhsT=pf[:, t, :],
-                    rhs=a_sb[:, 9 * rb + cb, 0:6 * nro].rearrange("p (r c) -> p r c", c=6),
-                    start=True, stop=True,
+                    out=spot[:, 0:nro, 6 * cc:6 * cc + 6], lhsT=pf[:, t, :],
+                    rhs=rhs.rearrange("p (r c) -> p r c", c=6), start=True, stop=True,
                 )
             if cc == 3:
-                dst = ag_all[:, 192 * rb:192 * rb + 192, :].rearrange("p (r w) t -> p r w t", w=IMG_W)
-                if rb < 9:
-                    pieces = [(0, 4, 24)]
-                elif half == 0:
-                    pieces = [(0, 1, 24), (1, 2, 16)]
+                row0 = 0 if c == 1 else 4 * c - 1
+                dst = ag_all[:, IMG_W * row0:IMG_W * (row0 + 7), :].rearrange("p (r w) t -> p r w t", w=IMG_W)
+                if c == 1:
+                    for u in range(2):
+                        nc.scalar.copy(
+                            out=dst[:, :, 24 * half:24 * half + 24, 2 * u:2 * u + 2],
+                            in_=later[("aggps", u)][:].rearrange("p t r c -> p r c t"),
+                        )
                 else:
-                    pieces = [(0, 1, 24)]
-                for ra, rz_, ncol in pieces:
-                    nc.scalar.copy(
-                        out=dst[:, ra:rz_, 24 * half:24 * half + ncol, :],
-                        in_=aggps[:, :, ra:rz_, 0:ncol].rearrange("p t r c -> p r c t"),
-                    )
+                    if c < 9:
+                        pieces = [(0, 4, 24)]
+                    elif half == 0:
+                        pieces = [(0, 2, 24), (2, 3, 16)]
+                    else:
+                        pieces = [(0, 2, 24)]
+                    for ra, rz_, ncol in pieces:
+                        nc.scalar.copy(
+                            out=dst[:, ra:rz_, 24 * half:24 * half + ncol, :],
+                            in_=later[("aggps", 0)][:, :, ra:rz_, 0:ncol].rearrange("p t r c -> p r c t"),
+                        )
                 if half == 1:
-                    ready = min(192 * (rb + 1), PE_PIX)
+                    ready = min(IMG_W * (4 * c + 3), PE_PIX)
                     while 256 * (later["chunk"] + 1) <= ready:
                         n0 = 256 * later["chunk"]
                         stage2(n0, ag_all[:, n0:n0 + 256, :].rearrange("p n t -> p (n t)"))
@@ -500,7 +537,7 @@ def tile_dcblock_kernel(tc, x, coarse_probs, sigma, w_feat, w_fuse, bn_gamma, bn
                 stage1_mm(1)
             if g == 5:
                 later["wu"] = prep_weight(wu_raw, "wu")
-        ag_all = work.tile([P, 1920, 4], BF16, name="ag_all", tag="big", align_bytes=64, bufs=1)
+        ag_all = work.tile([P, 2016, 4], BF16, name="ag_all", tag="big", align_bytes=64, bufs=1)
         later["chunk"] = 0
 
         e_items = []

@@ -28,8 +28,11 @@ PADP = 4
 PL = HW + 2 * PADP
 PK0 = 1784
 PKW = 528
-PITCH = 54
-PLW = 918
+PL_OFF = 4
+PL_ROWS = 54
+PLW = PL_OFF + IMG_W * PL_ROWS + 8
+CV_PAD = 72
+CV_PITCH = 168
 NPOS = 24
 E_SPAN = 64
 G_COUNT = 16
@@ -42,7 +45,6 @@ def tile_dcblock_kernel(tc, x, coarse_probs, sigma, w_feat, w_fuse, bn_gamma, bn
     x_v = x[0].rearrange("(p j) h w -> p j (h w)", j=4)
     out_v = out[0].rearrange("(m t) h w -> m t (h w)", t=4)
     cp_v = coarse_probs[0].rearrange("c h w -> c (h w)")
-    cp_r = coarse_probs[0].rearrange("c (b r) w -> c r b w", r=4)
     g_set = set(i for i in range(NOFF) if ((i + 1) * G_COUNT) // NOFF > (i * G_COUNT) // NOFF)
 
     with ExitStack() as ctx:
@@ -77,10 +79,14 @@ def tile_dcblock_kernel(tc, x, coarse_probs, sigma, w_feat, w_fuse, bn_gamma, bn
         warm = const.tile([P, 1], F32, name="warm")
         nc.scalar.activation(out=warm[:], in_=one[:], func=ACT.Sqrt)
 
-        pl_rows = pl[:, PITCH:PITCH + 12 * PITCH].rearrange("p (b w) -> p b w", w=PITCH)
-        for rr in range(4):
-            nc.sync.dma_start(out=pl_rows[CP * rr:CP * rr + 16, :, 4:4 + IMG_W], in_=cp_r[0:16, rr])
-            nc.scalar.dma_start(out=pl_rows[CP * rr + 16:CP * rr + CP, :, 4:4 + IMG_W], in_=cp_r[16:CP, rr])
+        for i in range(6):
+            r_lo = max(0, 3 - i)
+            r_hi = min(PL_ROWS, IMG_W + 3 - i)
+            dst0 = PL_OFF + IMG_W * r_lo
+            dst1 = PL_OFF + IMG_W * r_hi
+            src0 = IMG_W * (r_lo + i - 3)
+            nc.sync.dma_start(out=pl[CP * i:CP * i + 16, dst0:dst1], in_=cp_v[0:16, src0:src0 + dst1 - dst0])
+            nc.scalar.dma_start(out=pl[CP * i + 16:CP * i + CP, dst0:dst1], in_=cp_v[16:CP, src0:src0 + dst1 - dst0])
         nc.sync.dma_start(out=x_raw[:, :, 0:768], in_=x_v[:, :, 0:768])
         nc.sync.dma_start(out=wf_raw[:], in_=w_feat.rearrange("(m t) k -> m t k", t=4))
         nc.sync.dma_start(out=x_raw[:, :, 1536:2304], in_=x_v[:, :, 1536:2304])
@@ -105,8 +111,8 @@ def tile_dcblock_kernel(tc, x, coarse_probs, sigma, w_feat, w_fuse, bn_gamma, bn
         nc.gpsimd.memset(bands[:, :, :, 0:48], 0.0)
         nc.gpsimd.memset(bands[:, 0, :, :], 0.0)
         nc.gpsimd.memset(bands[:, 7, :, :], 0.0)
-        abig = work.tile([P, 3136], F32, name="abig", tag="big", align_bytes=64, bufs=1)
-        nc.vector.memset(abig[:], 0.0)
+        cv = const.tile([P, CV_PAD + 6 * (CV_PITCH + 1)], F32, name="cv")
+        nc.vector.memset(cv[:], 0.0)
         msg_e = const.tile([P, 4, ML], BF16, name="msg_e")
         msg_o = const.tile([P, 4, ML], BF16, name="msg_o")
         nc.vector.memset(msg_e[:, :, 760:ML], 0.0)
@@ -138,20 +144,28 @@ def tile_dcblock_kernel(tc, x, coarse_probs, sigma, w_feat, w_fuse, bn_gamma, bn
         nc.vector.reciprocal(out=neginv[:], in_=sg[:])
         nc.vector.tensor_scalar_mul(out=neginv[:], in0=neginv[:], scalar1=-1.0)
 
-        pz = const.tile([P, 10, 12, CP], BF16, name="pz")
-        for a in (-1, 0, 1):
-            for h in range(2):
-                pps = ps_pt.tile([P, 6, P], BF16, name="pps", tag="pt")
-                for j in range(6):
-                    s = PITCH * (1 + a) + 1 + 6 * h + j
-                    nc.tensor.transpose(pps[:, j, :], pl[:, s:s + 6 * (P - 1) + 1:6], ident_b[:])
-                rr0 = 0
-                rr1 = 2 if a == 1 else 4
-                ri0 = 4 * a + 4
-                nc.vector.tensor_copy(
-                    out=pz[:, ri0:ri0 + rr1 - rr0, 6 * h:6 * h + 6, :].rearrange("p r j c -> p j r c"),
-                    in_=pps[:, :, 0:4 * CP].rearrange("p j (r c) -> p j r c", c=CP)[:, :, rr0:rr1, :],
-                )
+        edge = const.tile([P, 2], F32, name="edge")
+        nc.vector.tensor_reduce(out=edge[:, 0:1], in_=ident_f[:, 0:P:8], axis=AX.X, op=ALU.add)
+        nc.vector.tensor_reduce(out=edge[:, 1:2], in_=ident_f[:, 7:P:8], axis=AX.X, op=ALU.add)
+        nc.vector.tensor_scalar(out=edge[:], in0=edge[:], scalar1=-1.0, scalar2=1.0, op0=ALU.mult, op1=ALU.add)
+        pz_of = {}
+
+        def pz_build(bt):
+            pz = affp.tile([P, KW, 12, CP], BF16, name="pz", tag="pz")
+            pz_of[bt] = pz
+            for far in range(2):
+                for h in range(2):
+                    pps = ps_pt.tile([P, 6, P], BF16, name="pps", tag="pt")
+                    for j in range(6):
+                        s = PL_OFF + IMG_W * (16 * bt + 6 * far) + 6 * h + j - 3
+                        nc.tensor.transpose(pps[:, j, :], pl[:, s:s + 6 * (P - 1) + 1:6], ident_b[:])
+                    nrow = 1 if far else 6
+                    nc.vector.tensor_copy(
+                        out=pz[:, 6 * far:6 * far + nrow, 6 * h:6 * h + 6, :].rearrange("p r j c -> p j r c"),
+                        in_=pps[:, :, 0:nrow * CP].rearrange("p j (r c) -> p j r c", c=CP),
+                    )
+            nc.vector.tensor_scalar(out=pz[:, :, 0:3, :], in0=pz[:, :, 0:3, :], scalar1=edge[:, 0:1], scalar2=None, op0=ALU.mult)
+            nc.vector.tensor_scalar(out=pz[:, :, 9:12, :], in0=pz[:, :, 9:12, :], scalar1=edge[:, 1:2], scalar2=None, op0=ALU.mult)
 
         def prep_weight(raw, label):
             grouped = work.tile([P, 4 * C], BF16, name="grouped", tag="grouped", align_bytes=64, bufs=1)
@@ -221,72 +235,74 @@ def tile_dcblock_kernel(tc, x, coarse_probs, sigma, w_feat, w_fuse, bn_gamma, bn
         stage1_quant(0)
         stage1_mm(0)
 
-        dist = const.tile([P, NPOS * NOFF], F32, name="dist")
-        zs_p = const.tile([P, NPOS], F32, name="zs_p")
-        rz_p = const.tile([P, NPOS], F32, name="rz_p")
         a_sb = const.tile([P, 90, NPOS], F32, name="a_sb")
         a_top = const.tile([P, 8, 42], F32, name="a_top")
-        atop = const.tile([P, 18 * P + 64], F32, name="atop")
-        nc.vector.memset(atop[:], 0.0)
+        row_bands = [(0, 7, 0)] + [(4 * c - 1, 4 if c < 9 else 3, 4 * c - 4) for c in range(2, 10)]
+        shift_of = {}
+        for r0, nro, w0 in row_bands:
+            for r in range(r0, r0 + nro):
+                shift_of[r] = r - 3 - w0
+        dist_of = {}
 
-        def a_group(g):
+        def a_group(bt, g):
+            pz = pz_of[bt]
+            if g == 0:
+                dist_of[bt] = affp.tile([P, 6 * NOFF], F32, name="dist", tag="dist")
             pdiff = affp.tile([P, 3, NOFF * CP], F32, name="pdiff", tag="diff")
             for i in range(3):
-                ro, co = divmod(3 * g + i, 6)
+                co = 3 * g + i
                 nc.gpsimd.tensor_tensor(
                     out=pdiff[:, i, :].rearrange("p (d e c) -> p d e c", d=KW, c=CP),
-                    in0=pz[:, ro:ro + KW, co:co + KW, :],
-                    in1=pz[:, ro + 3:ro + 4, co + 3:co + 4, :].to_broadcast([P, KW, KW, CP]),
+                    in0=pz[:, :, co:co + KW, :],
+                    in1=pz[:, 3:4, co + 3:co + 4, :].to_broadcast([P, KW, KW, CP]),
                     op=ALU.subtract,
                 )
             flat = pdiff[:].rearrange("p i f -> p (i f)")
             nc.scalar.activation(out=flat, in_=flat, func=ACT.Square)
             nc.vector.tensor_reduce(
-                out=dist[:, 3 * NOFF * g:3 * NOFF * (g + 1)],
+                out=dist_of[bt][:, 3 * NOFF * g:3 * NOFF * (g + 1)],
                 in_=pdiff[:].rearrange("p i (f c) -> p (i f) c", c=CP), axis=AX.X, op=ALU.add,
             )
 
-        def a_finish(ro):
-            d6 = dist[:, 6 * NOFF * ro:6 * NOFF * (ro + 1)]
+        def a_finish(bt):
+            d6 = dist_of[bt][:]
             nc.scalar.activation(out=d6, in_=d6, func=ACT.Exp, scale=neginv[:, 0:1])
             nc.scalar.activation(out=d6, in_=d6, func=ACT.Exp, bias=-1.0)
-            nc.vector.tensor_reduce(
-                out=zs_p[:, 6 * ro:6 * ro + 6], in_=d6.rearrange("p (n f) -> p n f", f=NOFF), axis=AX.X, op=ALU.add,
-            )
-            nc.vector.reciprocal(out=rz_p[:, 6 * ro:6 * ro + 6], in_=zs_p[:, 6 * ro:6 * ro + 6])
-            s0 = ro * (6 * P + 12)
-            canvas = abig[:, s0:s0 + 6 * (P + 1)].rearrange("p (a x) -> p a x", x=P + 1)[:, :, 0:84]
+            zs_p = affp.tile([P, 6], F32, name="zs_p", tag="zs_p")
+            rz_p = affp.tile([P, 6], F32, name="rz_p", tag="rz_p")
+            nc.vector.tensor_reduce(out=zs_p[:], in_=d6.rearrange("p (n f) -> p n f", f=NOFF), axis=AX.X, op=ALU.add)
+            nc.vector.reciprocal(out=rz_p[:], in_=zs_p[:])
+            canvas = cv[:, CV_PAD:CV_PAD + 6 * (CV_PITCH + 1)].rearrange("p (a x) -> p a x", x=CV_PITCH + 1)[:, :, 0:84]
             nc.vector.tensor_tensor(
                 out=canvas.rearrange("p a (d e) -> p a d e", e=12)[:, :, :, 0:KW],
                 in0=d6.rearrange("p (a d e) -> p a d e", d=KW, e=KW),
-                in1=rz_p[:, 6 * ro:6 * ro + 6].unsqueeze(2).unsqueeze(3).to_broadcast([P, 6, KW, KW]),
+                in1=rz_p[:].unsqueeze(2).unsqueeze(3).to_broadcast([P, 6, KW, KW]),
                 op=ALU.mult,
             )
-            for u in range(2):
-                n0 = 6 * ro + 3 * u
-                aps = ps_agg.tile([P, 3, P], F32, name="aps", tag="agg")
-                for j in range(3):
-                    nc.tensor.transpose(aps[:, j, :], abig[:, P * (n0 + j):P * (n0 + j) + P], ident_f[:])
-                nc.scalar.copy(out=a_sb[:, :, n0:n0 + 3], in_=aps[:, :, 0:90].rearrange("p j q -> p q j"))
-            if ro == 0:
-                return
-            nd = ro + 3
-            t0 = (ro - 1) * 6 * P
-            canvas = atop[:, t0:t0 + 6 * (P + 1)].rearrange("p (a x) -> p a x", x=P + 1)[:, :, 0:12 * nd]
-            nc.vector.tensor_tensor(
-                out=canvas.rearrange("p a (d e) -> p a d e", e=12)[:, :, :, 0:KW],
-                in0=d6.rearrange("p (a d e) -> p a d e", d=KW, e=KW)[:, :, KW - nd:KW, :],
-                in1=rz_p[:, 6 * ro:6 * ro + 6].unsqueeze(2).unsqueeze(3).to_broadcast([P, 6, nd, KW]),
-                op=ALU.mult,
-            )
-            for u in range(2):
-                n0 = 6 * (ro - 1) + 3 * u
-                aps = ps_agg.tile([P, 3, P], F32, name="aps", tag="agg")
-                for j in range(3):
-                    nc.tensor.transpose(aps[:, j, :], atop[:, P * (n0 + j):P * (n0 + j) + P], ident_f[:])
-                nc.scalar.copy(out=a_top[:, :, n0:n0 + 3], in_=aps[:, :, 0:8].rearrange("p j q -> p q j"))
-            if ro == 3:
-                nc.scalar.copy(out=a_top[:, :, 18:42], in_=a_sb[:, 9:17, :])
+            rows_of = {}
+            for r in range(16 * bt, 16 * bt + 16):
+                if r in shift_of:
+                    rows_of.setdefault(shift_of[r], []).append(r)
+            for sh in sorted(rows_of):
+                rows = rows_of[sh]
+                low = [r for r in rows if r >= 7]
+                assert all(low[i + 1] - low[i] == 4 for i in range(len(low) - 1))
+                for u in range(2):
+                    aps = ps_agg.tile([P, 3, P], F32, name="aps", tag="agg")
+                    for j in range(3):
+                        s = CV_PAD + CV_PITCH * (3 * u + j) - 12 * sh
+                        nc.tensor.transpose(aps[:, j, :], cv[:, s:s + P], ident_f[:])
+                    lines = aps[:].rearrange("p j (r b) -> p j r b", b=8)
+                    if rows[0] < 7:
+                        n0 = 6 * rows[0] + 3 * u
+                        nc.scalar.copy(out=a_top[:, :, n0:n0 + 3].rearrange("p b j -> p j b"), in_=lines[:, :, rows[0] - 16 * bt, :])
+                    if low:
+                        c0 = (low[0] + 1) // 4
+                        n0 = 6 * sh + 3 * u
+                        nc.scalar.copy(
+                            out=a_sb[:, 9 * c0:9 * (c0 + len(low)), n0:n0 + 3].rearrange("p (c b) j -> p j c b", b=9)[:, :, :, 0:8],
+                            in_=lines[:, :, low[0] - 16 * bt:low[-1] - 16 * bt + 1:4, :],
+                        )
 
         NT = 2 * len(E_PAIRS)
         n_i = const.tile([P, NT], I32, name="n_i")
@@ -520,22 +536,26 @@ def tile_dcblock_kernel(tc, x, coarse_probs, sigma, w_feat, w_fuse, bn_gamma, bn
 
         first, second = E_PAIRS
         stage1_quant(2)
-        a_group(0)
+        pz_build(2)
+        a_group(2, 0)
         stage1_mm(2)
         affinity(first)
         e_begin(first)
-        for g in range(8):
+        groups = [(2, 0), (2, 1), (1, 0), (1, 1), (0, 0), (0, 1)]
+        for g, (bt, half) in enumerate(groups):
             if g > 0:
-                a_group(g)
-            if g % 2 == 1:
-                a_finish(g // 2)
-            for f in range((g * HEAD_STEPS) // 8, ((g + 1) * HEAD_STEPS) // 8):
+                a_group(bt, half)
+            if half == 0 and bt > 0:
+                pz_build(bt - 1)
+            if half == 1:
+                a_finish(bt)
+            for f in range((g * HEAD_STEPS) // 6, ((g + 1) * HEAD_STEPS) // 6):
                 e_step(first, f)
-            if g == 2:
+            if g == 1:
                 stage1_quant(1)
-            if g == 3:
+            if g == 2:
                 stage1_mm(1)
-            if g == 5:
+            if g == 4:
                 later["wu"] = prep_weight(wu_raw, "wu")
         ag_all = work.tile([P, 2016, 4], BF16, name="ag_all", tag="big", align_bytes=64, bufs=1)
         later["chunk"] = 0

@@ -160,7 +160,7 @@ def tile_dcblock_kernel(tc, x, coarse_probs, sigma, w_feat, w_fuse, bn_gamma, bn
                         s = PL_OFF + IMG_W * (16 * bt + 6 * far) + 6 * h + j - 3
                         nc.tensor.transpose(pps[:, j, :], pl[:, s:s + 6 * (P - 1) + 1:6], ident_b[:])
                     nrow = 1 if far else 6
-                    nc.vector.tensor_copy(
+                    nc.scalar.copy(
                         out=pz[:, 6 * far:6 * far + nrow, 6 * h:6 * h + 6, :].rearrange("p r j c -> p j r c"),
                         in_=pps[:, :, 0:nrow * CP].rearrange("p j (r c) -> p j r c", c=CP),
                     )
@@ -440,7 +440,7 @@ def tile_dcblock_kernel(tc, x, coarse_probs, sigma, w_feat, w_fuse, bn_gamma, bn
                 nc.tensor.transpose(win[:, P * t:P * t + P], src[:, t, :].bitcast(F32)[:, word0:word0 + P], ident_f[:])
             halves = win[:].bitcast(BF16)
             acg = later[("acg", pi)]
-            on_g = [i for i in range(NOFF) if i in g_set and not (pi == E_PAIRS[0] and i < HEAD_STEPS)]
+            on_g = [i for i in range(NOFF) if i in g_set]
             first_g = f == min(on_g)
             first_v = f == min(i for i in range(NOFF) if i not in on_g)
             if f in on_g:
@@ -536,17 +536,17 @@ def tile_dcblock_kernel(tc, x, coarse_probs, sigma, w_feat, w_fuse, bn_gamma, bn
 
         first, second = E_PAIRS
         stage1_quant(2)
-        pz_build(2)
-        a_group(2, 0)
+        pz_build(0)
+        a_group(0, 0)
         stage1_mm(2)
         affinity(first)
         e_begin(first)
-        groups = [(2, 0), (2, 1), (1, 0), (1, 1), (0, 0), (0, 1)]
+        groups = [(0, 0), (0, 1), (1, 0), (1, 1), (2, 0), (2, 1)]
         for g, (bt, half) in enumerate(groups):
             if g > 0:
                 a_group(bt, half)
-            if half == 0 and bt > 0:
-                pz_build(bt - 1)
+            if half == 0 and bt < 2:
+                pz_build(bt + 1)
             if half == 1:
                 a_finish(bt)
             for f in range((g * HEAD_STEPS) // 6, ((g + 1) * HEAD_STEPS) // 6):

from contextlib import ExitStack

import concourse.masks as masks
import concourse.mybir as mybir

F32 = mybir.dt.float32
BF16 = mybir.dt.bfloat16
U32 = mybir.dt.uint32
U8 = mybir.dt.uint8
I32 = mybir.dt.int32
FP8X4 = mybir.dt.float8_e4m3fn_x4
ALU = mybir.AluOpType
ACT = mybir.ActivationFunctionType
AX = mybir.AxisListType

P = 128
C = 512
CP = 19
IMG_W = 48
HW = 2304
KW = 7
NOFF = 49
PE_PIX = 1792
E_PAIRS = (7, 8)
ME0 = 1536
ML = 928
PADP = 4
PL = HW + 2 * PADP
PK0 = 1784
PKW = 528
PL_OFF = 4
PL_ROWS = 54
PLW = PL_OFF + IMG_W * PL_ROWS + 8
CV_PAD = 72
CV_PITCH = 168
NPOS = 24
E_SPAN = 64
G_COUNT = 16
HEAD_STEPS = 30
FLOPS = 2 * 2 * C * C * HW + 2 * NOFF * C * HW + 3 * NOFF * CP * HW


def tile_dcblock_kernel(tc, x, coarse_probs, sigma, w_feat, w_fuse, bn_gamma, bn_beta, bn_mean, bn_var, out):
    nc = tc.nc
    x_v = x[0].rearrange("(p j) h w -> p j (h w)", j=4)
    out_v = out[0].rearrange("(m t) h w -> m t (h w)", t=4)
    cp_v = coarse_probs[0].rearrange("c h w -> c (h w)")
    g_set = set(i for i in range(NOFF) if ((i + 1) * G_COUNT) // NOFF > (i * G_COUNT) // NOFF)

    with ExitStack() as ctx:
        const = ctx.enter_context(tc.tile_pool(name="const", bufs=1))
        work = ctx.enter_context(tc.tile_pool(name="work", bufs=2))
        affp = ctx.enter_context(tc.tile_pool(name="affp", bufs=2))
        ps_win = ctx.enter_context(tc.psum_pool(name="ps_win", bufs=2))
        ps_pt = ctx.enter_context(tc.psum_pool(name="ps_pt", bufs=2))
        ps_agg = ctx.enter_context(tc.psum_pool(name="ps_agg", bufs=2))
        ps_aux = ctx.enter_context(tc.psum_pool(name="ps_aux", bufs=2))

        pl = const.tile([P, PLW], BF16, name="pl")
        nc.vector.memset(pl[:], 0.0)
        one = const.tile([P, 1], F32, name="one")
        nc.vector.memset(one[:], 1.0)
        pk_a = const.tile([P, PKW], BF16, name="pk_a")
        pk_b = const.tile([P, PKW], BF16, name="pk_b")
        nc.vector.memset(pk_a[:], 0.0)
        nc.vector.memset(pk_b[:], 0.0)
        x_raw = const.tile([P, 4, HW], BF16, name="x_raw")
        wf_raw = work.tile([P, 4, C], BF16, name="wf_raw", tag="w_raw", bufs=1)
        gam = const.tile([P, 4], BF16, name="gam")
        bet = const.tile([P, 4], BF16, name="bet")
        mea = const.tile([P, 4], BF16, name="mea")
        var = const.tile([P, 4], BF16, name="var")
        sig = const.tile([P, 1], BF16, name="sig")
        nc.scalar.dma_start(out=var[:], in_=bn_var.rearrange("(p j) -> p j", j=4))
        nc.scalar.dma_start(out=gam[:], in_=bn_gamma.rearrange("(p j) -> p j", j=4))
        nc.scalar.dma_start(out=mea[:], in_=bn_mean.rearrange("(p j) -> p j", j=4))
        nc.scalar.dma_start(out=bet[:], in_=bn_beta.rearrange("(p j) -> p j", j=4))
        nc.scalar.dma_start(out=sig[:], in_=sigma.partition_broadcast(P))
        warm = const.tile([P, 1], F32, name="warm")
        nc.scalar.activation(out=warm[:], in_=one[:], func=ACT.Sqrt)

        for i in range(6):
            r_lo = max(0, 3 - i)
            r_hi = min(PL_ROWS, IMG_W + 3 - i)
            dst0 = PL_OFF + IMG_W * r_lo
            dst1 = PL_OFF + IMG_W * r_hi
            src0 = IMG_W * (r_lo + i - 3)
            nc.sync.dma_start(out=pl[CP * i:CP * i + 16, dst0:dst1], in_=cp_v[0:16, src0:src0 + dst1 - dst0])
            nc.scalar.dma_start(out=pl[CP * i + 16:CP * i + CP, dst0:dst1], in_=cp_v[16:CP, src0:src0 + dst1 - dst0])
        nc.sync.dma_start(out=x_raw[:, :, 0:768], in_=x_v[:, :, 0:768])
        nc.sync.dma_start(out=wf_raw[:], in_=w_feat.rearrange("(m t) k -> m t k", t=4))
        nc.sync.dma_start(out=x_raw[:, :, 1536:2304], in_=x_v[:, :, 1536:2304])
        for dix in range(KW):
            di = dix - 3
            pk = pk_a if dix < 4 else pk_b
            s = dix if dix < 4 else dix - 4
            q_lo = max(PK0, PADP - IMG_W * di)
            q_hi = min(PL, HW + PADP - IMG_W * di)
            n_lo = q_lo - PADP + IMG_W * di
            n_hi = q_hi - PADP + IMG_W * di
            nc.sync.dma_start(out=pk[CP * s:CP * s + 16, q_lo - PK0:q_hi - PK0], in_=cp_v[0:16, n_lo:n_hi])
            nc.scalar.dma_start(out=pk[CP * s + 16:CP * s + CP, q_lo - PK0:q_hi - PK0], in_=cp_v[16:CP, n_lo:n_hi])
        nc.sync.dma_start(out=x_raw[:, :, 768:1536], in_=x_v[:, :, 768:1536])

        ident_b = const.tile([P, P], BF16, name="ident_b")
        masks.make_identity(nc, ident_b[:])
        ident_f = const.tile([P, P], F32, name="ident_f")
        masks.make_identity(nc, ident_f[:])

        bands = const.tile([P, 8, 4, 576], BF16, name="bands")
        nc.gpsimd.memset(bands[:, :, :, 0:48], 0.0)
        nc.gpsimd.memset(bands[:, 0, :, :], 0.0)
        nc.gpsimd.memset(bands[:, 7, :, :], 0.0)
        cv = const.tile([P, CV_PAD + 6 * (CV_PITCH + 1)], F32, name="cv")
        nc.vector.memset(cv[:], 0.0)
        msg_e = const.tile([P, 4, ML], BF16, name="msg_e")
        msg_o = const.tile([P, 4, ML], BF16, name="msg_o")
        nc.vector.memset(msg_e[:, :, 760:ML], 0.0)
        nc.vector.memset(msg_o[:, :, 760:ML], 0.0)

        v1 = const.tile([P, 4], F32, name="v1")
        nc.vector.tensor_scalar_add(out=v1[:], in0=var[:], scalar1=1e-5)
        sq = const.tile([P, 4], F32, name="sq")
        nc.scalar.activation(out=sq[:], in_=v1[:], func=ACT.Sqrt)
        nc.scalar.activation(out=warm[:], in_=one[:], func=ACT.Exp)
        r0 = const.tile([P, 4], F32, name="r0")
        nc.vector.reciprocal(out=r0[:], in_=sq[:])
        nt = const.tile([P, 4], F32, name="nt")
        nc.vector.tensor_tensor(out=nt[:], in0=r0[:], in1=r0[:], op=ALU.mult)
        nc.vector.tensor_tensor(out=nt[:], in0=nt[:], in1=v1[:], op=ALU.mult)
        nc.vector.tensor_scalar(out=nt[:], in0=nt[:], scalar1=-0.5, scalar2=1.5, op0=ALU.mult, op1=ALU.add)
        nc.vector.tensor_tensor(out=nt[:], in0=nt[:], in1=r0[:], op=ALU.mult)
        bn_s = const.tile([P, 4], F32, name="bn_s")
        nc.vector.tensor_tensor(out=bn_s[:], in0=nt[:], in1=gam[:], op=ALU.mult)
        bn_b = const.tile([P, 4], F32, name="bn_b")
        nc.vector.tensor_tensor(out=bn_b[:], in0=bn_s[:], in1=mea[:], op=ALU.mult)
        nc.vector.tensor_tensor(out=bn_b[:], in0=bet[:], in1=bn_b[:], op=ALU.subtract)

        sg = const.tile([P, 1], F32, name="sg")
        nc.vector.tensor_scalar_max(out=sg[:], in0=sig[:], scalar1=0.0)
        nc.vector.tensor_tensor(out=sg[:], in0=sg[:], in1=sg[:], op=ALU.mult)
        nc.vector.tensor_scalar(out=sg[:], in0=sg[:], scalar1=2.0, scalar2=1e-8, op0=ALU.mult, op1=ALU.add)
        neginv = const.tile([P, 1], F32, name="neginv")
        nc.vector.reciprocal(out=neginv[:], in_=sg[:])
        nc.vector.tensor_scalar_mul(out=neginv[:], in0=neginv[:], scalar1=-1.0)

        edge = const.tile([P, 2], F32, name="edge")
        nc.vector.tensor_reduce(out=edge[:, 0:1], in_=ident_f[:, 0:P:8], axis=AX.X, op=ALU.add)
        nc.vector.tensor_reduce(out=edge[:, 1:2], in_=ident_f[:, 7:P:8], axis=AX.X, op=ALU.add)
        nc.vector.tensor_scalar(out=edge[:], in0=edge[:], scalar1=-1.0, scalar2=1.0, op0=ALU.mult, op1=ALU.add)
        pz_of = {}

        def pz_build(bt):
            pz = affp.tile([P, KW, 12, CP], BF16, name="pz", tag="pz")
            pz_of[bt] = pz
            for far in range(2):
                for h in range(2):
                    pps = ps_pt.tile([P, 6, P], BF16, name="pps", tag="pt")
                    for j in range(6):
                        s = PL_OFF + IMG_W * (16 * bt + 6 * far) + 6 * h + j - 3
                        nc.tensor.transpose(pps[:, j, :], pl[:, s:s + 6 * (P - 1) + 1:6], ident_b[:])
                    nrow = 1 if far else 6
                    nc.scalar.copy(
                        out=pz[:, 6 * far:6 * far + nrow, 6 * h:6 * h + 6, :].rearrange("p r j c -> p j r c"),
                        in_=pps[:, :, 0:nrow * CP].rearrange("p j (r c) -> p j r c", c=CP),
                    )
            nc.vector.tensor_scalar(out=pz[:, :, 0:3, :], in0=pz[:, :, 0:3, :], scalar1=edge[:, 0:1], scalar2=None, op0=ALU.mult)
            nc.vector.tensor_scalar(out=pz[:, :, 9:12, :], in0=pz[:, :, 9:12, :], scalar1=edge[:, 1:2], scalar2=None, op0=ALU.mult)

        def prep_weight(raw, label):
            grouped = work.tile([P, 4 * C], BF16, name="grouped", tag="grouped", align_bytes=64, bufs=1)
            gw = grouped[:].bitcast(F32).rearrange("p (t m u) -> p t m u", t=4, u=2)
            for half in range(2):
                ps = ps_aux.tile([P, 2, 2, P], F32, name=label + "_ps", tag="aux")
                for tt in range(2):
                    words = raw[:, 2 * half + tt, :].bitcast(F32)
                    for u in range(2):
                        nc.tensor.transpose(ps[:, tt, u, :], words[:, u::2], ident_f[:])
                nc.vector.tensor_copy(out=gw[:, 2 * half:2 * half + 2], in_=ps[:].rearrange("p t u m -> p t m u"))
            codes = const.tile([P, C], U32, name=label + "_codes", align_bytes=64)
            scl = const.tile([P, C], U8, name=label + "_scl", align_bytes=64)
            nc.vector.quantize_mx(out=codes[:].bitcast(FP8X4), scales=scl[:], in_=grouped[:])
            return codes, scl

        wf_codes, wf_scl = prep_weight(wf_raw, "wf")
        wu_raw = work.tile([P, 4, C], BF16, name="wu_raw", tag="w_raw", bufs=1)
        nc.sync.dma_start(out=wu_raw[:], in_=w_fuse.rearrange("(m t) k -> m t k", t=4))

        x_codes = const.tile([P, HW], U32, name="x_codes", align_bytes=64)
        x_scl = const.tile([P, HW], U8, name="x_scl", align_bytes=64)

        def stage1_quant(g):
            c0 = 768 * g
            xn = work.tile([P, 4, 768], BF16, name="xn", tag="x2", align_bytes=64)
            xg = work.tile([P, 768, 4], BF16, name="xg", tag="x2", align_bytes=64)
            eng = nc.vector
            for j in range(4):
                eng.tensor_scalar(
                    out=xn[:, j, :], in0=x_raw[:, j, c0:c0 + 768],
                    scalar1=bn_s[:, j:j + 1], scalar2=bn_b[:, j:j + 1], op0=ALU.mult, op1=ALU.add,
                )
            eng.tensor_copy(out=xg[:], in_=xn[:].rearrange("p j n -> p n j"))
            for u in range(3):
                n0 = c0 + 256 * u
                nc.vector.quantize_mx(
                    out=x_codes[:, n0:n0 + 256].bitcast(FP8X4), scales=x_scl[:, n0:n0 + 256],
                    in_=xg[:, 256 * u:256 * u + 256, :].rearrange("p n j -> p (n j)"),
                )

        def stage1_mm(g):
            c0 = 768 * g
            nr = 16 if g < 2 else 12
            b0 = 12 * (16 * g + 3)
            for t in range(4):
                bank = ps_aux.tile([P, 3, 256], BF16, name="bank", tag="aux")
                for h in range(3):
                    n0 = c0 + 256 * h
                    nc.tensor.matmul_mx(
                        out=bank[:, h, :],
                        lhsT=wf_codes[:, P * t:P * t + P].bitcast(FP8X4), lhsT_scale=wf_scl[:, P * t:P * t + P],
                        rhs=x_codes[:, n0:n0 + 256].bitcast(FP8X4), rhs_scale=x_scl[:, n0:n0 + 256],
                        start=True, stop=True,
                    )
                flat = bank[:].rearrange("p h n -> p (h n)")
                rows = flat.rearrange("p (r w) -> p r w", w=IMG_W)
                dst = bands[:, :, t, b0:b0 + 12 * nr].rearrange("p b (r i) -> p b r i", i=12)
                nc.scalar.copy(out=dst[:, 1:6:2], in_=rows[:, 0:nr, 3:39].rearrange("p r (b i) -> p b r i", i=12))
                nc.scalar.copy(out=dst[:, 2:7:2], in_=rows[:, 0:nr, 9:45].rearrange("p r (b i) -> p b r i", i=12))
                nc.scalar.copy(out=dst[:, 0, :, 3:12], in_=rows[:, 0:nr, 0:9])
                nc.scalar.copy(out=dst[:, 7, :, 0:9], in_=rows[:, 0:nr, 39:48])
                if g == 2:
                    nc.scalar.copy(out=msg_e[:, t, 0:768], in_=flat)
                    nc.scalar.copy(out=msg_o[:, t, 0:767], in_=flat[:, 1:768])

        stage1_quant(0)
        stage1_mm(0)

        a_sb = const.tile([P, 90, NPOS], F32, name="a_sb")
        a_top = const.tile([P, 8, 42], F32, name="a_top")
        row_bands = [(0, 7, 0)] + [(4 * c - 1, 4 if c < 9 else 3, 4 * c - 4) for c in range(2, 10)]
        shift_of = {}
        for r0, nro, w0 in row_bands:
            for r in range(r0, r0 + nro):
                shift_of[r] = r - 3 - w0
        dist_of = {}

        def a_group(bt, g):
            pz = pz_of[bt]
            if g == 0:
                dist_of[bt] = affp.tile([P, 6 * NOFF], F32, name="dist", tag="dist")
            pdiff = affp.tile([P, 3, NOFF * CP], F32, name="pdiff", tag="diff")
            for i in range(3):
                co = 3 * g + i
                nc.gpsimd.tensor_tensor(
                    out=pdiff[:, i, :].rearrange("p (d e c) -> p d e c", d=KW, c=CP),
                    in0=pz[:, :, co:co + KW, :],
                    in1=pz[:, 3:4, co + 3:co + 4, :].to_broadcast([P, KW, KW, CP]),
                    op=ALU.subtract,
                )
            flat = pdiff[:].rearrange("p i f -> p (i f)")
            nc.scalar.activation(out=flat, in_=flat, func=ACT.Square)
            nc.vector.tensor_reduce(
                out=dist_of[bt][:, 3 * NOFF * g:3 * NOFF * (g + 1)],
                in_=pdiff[:].rearrange("p i (f c) -> p (i f) c", c=CP), axis=AX.X, op=ALU.add,
            )

        def a_finish(bt):
            d6 = dist_of[bt][:]
            nc.scalar.activation(out=d6, in_=d6, func=ACT.Exp, scale=neginv[:, 0:1])
            nc.scalar.activation(out=d6, in_=d6, func=ACT.Exp, bias=-1.0)
            zs_p = affp.tile([P, 6], F32, name="zs_p", tag="zs_p")
            rz_p = affp.tile([P, 6], F32, name="rz_p", tag="rz_p")
            nc.vector.tensor_reduce(out=zs_p[:], in_=d6.rearrange("p (n f) -> p n f", f=NOFF), axis=AX.X, op=ALU.add)
            nc.vector.reciprocal(out=rz_p[:], in_=zs_p[:])
            canvas = cv[:, CV_PAD:CV_PAD + 6 * (CV_PITCH + 1)].rearrange("p (a x) -> p a x", x=CV_PITCH + 1)[:, :, 0:84]
            nc.vector.tensor_tensor(
                out=canvas.rearrange("p a (d e) -> p a d e", e=12)[:, :, :, 0:KW],
                in0=d6.rearrange("p (a d e) -> p a d e", d=KW, e=KW),
                in1=rz_p[:].unsqueeze(2).unsqueeze(3).to_broadcast([P, 6, KW, KW]),
                op=ALU.mult,
            )
            rows_of = {}
            for r in range(16 * bt, 16 * bt + 16):
                if r in shift_of:
                    rows_of.setdefault(shift_of[r], []).append(r)
            for sh in sorted(rows_of):
                rows = rows_of[sh]
                low = [r for r in rows if r >= 7]
                assert all(low[i + 1] - low[i] == 4 for i in range(len(low) - 1))
                for u in range(2):
                    aps = ps_agg.tile([P, 3, P], F32, name="aps", tag="agg")
                    for j in range(3):
                        s = CV_PAD + CV_PITCH * (3 * u + j) - 12 * sh
                        nc.tensor.transpose(aps[:, j, :], cv[:, s:s + P], ident_f[:])
                    lines = aps[:].rearrange("p j (r b) -> p j r b", b=8)
                    if rows[0] < 7:
                        n0 = 6 * rows[0] + 3 * u
                        nc.scalar.copy(out=a_top[:, :, n0:n0 + 3].rearrange("p b j -> p j b"), in_=lines[:, :, rows[0] - 16 * bt, :])
                    if low:
                        c0 = (low[0] + 1) // 4
                        n0 = 6 * sh + 3 * u
                        nc.scalar.copy(
                            out=a_sb[:, 9 * c0:9 * (c0 + len(low)), n0:n0 + 3].rearrange("p (c b) j -> p j c b", b=9)[:, :, :, 0:8],
                            in_=lines[:, :, low[0] - 16 * bt:low[-1] - 16 * bt + 1:4, :],
                        )

        NT = 2 * len(E_PAIRS)
        n_i = const.tile([P, NT], I32, name="n_i")
        nc.gpsimd.iota(n_i[:], pattern=[[2 * P, len(E_PAIRS)], [1, 2]], base=PE_PIX, channel_multiplier=2)
        thr_i = const.tile([P, IMG_W - 1], I32, name="thr_i")
        nc.gpsimd.iota(thr_i[:], pattern=[[IMG_W, IMG_W - 1]], base=IMG_W, channel_multiplier=0)
        dj_i = const.tile([P, KW], I32, name="dj_i")
        nc.gpsimd.iota(dj_i[:], pattern=[[1, KW]], base=-3, channel_multiplier=0)
        n_f = const.tile([P, NT], F32, name="n_f")
        nc.vector.tensor_copy(out=n_f[:], in_=n_i[:])
        thr_f = const.tile([P, IMG_W - 1], F32, name="thr_f")
        nc.vector.tensor_copy(out=thr_f[:], in_=thr_i[:])
        dj_f = const.tile([P, KW], F32, name="dj_f")
        nc.vector.tensor_copy(out=dj_f[:], in_=dj_i[:])
        cmp = const.tile([P, NT, IMG_W - 1], F32, name="cmp")
        nc.vector.tensor_tensor(
            out=cmp[:],
            in0=n_f[:].unsqueeze(2).to_broadcast([P, NT, IMG_W - 1]),
            in1=thr_f[:].unsqueeze(1).to_broadcast([P, NT, IMG_W - 1]),
            op=ALU.is_ge,
        )
        row = const.tile([P, NT], F32, name="row")
        nc.vector.tensor_reduce(out=row[:], in_=cmp[:], axis=AX.X, op=ALU.add)
        col = const.tile([P, NT], F32, name="col")
        nc.vector.scalar_tensor_tensor(out=col[:], in0=row[:], scalar=-48.0, in1=n_f[:], op0=ALU.mult, op1=ALU.add)
        cj = const.tile([P, NT, KW], F32, name="cj")
        nc.vector.tensor_tensor(
            out=cj[:],
            in0=col[:].unsqueeze(2).to_broadcast([P, NT, KW]),
            in1=dj_f[:].unsqueeze(1).to_broadcast([P, NT, KW]),
            op=ALU.add,
        )
        m_lo = const.tile([P, NT, KW], F32, name="m_lo")
        nc.vector.tensor_scalar(out=m_lo[:], in0=cj[:], scalar1=0.0, scalar2=None, op0=ALU.is_ge)
        mask7 = const.tile([P, NT, KW], F32, name="mask7")
        nc.vector.scalar_tensor_tensor(
            out=mask7[:].rearrange("p t j -> p (t j)"),
            in0=cj[:].rearrange("p t j -> p (t j)"),
            scalar=47.0,
            in1=m_lo[:].rearrange("p t j -> p (t j)"),
            op0=ALU.is_le,
            op1=ALU.mult,
        )
        cnt = const.tile([P, NT], F32, name="cnt")
        nc.vector.tensor_reduce(out=cnt[:], in_=mask7[:], axis=AX.X, op=ALU.add)
        nc.vector.tensor_scalar(out=cnt[:], in0=cnt[:], scalar1=-7.0, scalar2=49.0, op0=ALU.mult, op1=ALU.add)
        mask49 = const.tile([P, NT, KW, KW], F32, name="mask49")
        nc.vector.tensor_copy(out=mask49[:], in_=mask7[:].unsqueeze(3).to_broadcast([P, NT, KW, KW]))

        later = {}

        def affinity(pi):
            pp = pi - E_PAIRS[0]
            diff = affp.tile([P, 2, NOFF + 1, CP], F32, name="diff", tag="diff")
            for a in range(2):
                n0 = PADP + 2 * P * pi + a - 3 - PK0
                win_a = ps_aux.tile([P, KW, P], BF16, name="win_a", tag="aux")
                win_b = ps_aux.tile([P, KW, P], BF16, name="win_b", tag="aux")
                for djx in range(KW):
                    nc.tensor.transpose(win_a[:, djx, :], pk_a[:, n0 + djx:n0 + djx + 2 * P:2], ident_b[:])
                for djx in range(KW):
                    nc.tensor.transpose(win_b[:, djx, :], pk_b[:, n0 + djx:n0 + djx + 2 * P:2], ident_b[:])
                nc.scalar.copy(out=diff[:, a, NOFF, :], in_=win_a[:, 3, 3 * CP:4 * CP])
                dv = diff[:, a, 0:NOFF, :].rearrange("p (j i) c -> p j i c", i=KW)
                centre = diff[:, a, NOFF:NOFF + 1, :].unsqueeze(1)
                nc.vector.tensor_tensor(
                    out=dv[:, :, 0:4, :], in0=win_a[:, :, 0:4 * CP].rearrange("p j (i c) -> p j i c", c=CP),
                    in1=centre.to_broadcast([P, KW, 4, CP]), op=ALU.subtract,
                )
                nc.vector.tensor_tensor(
                    out=dv[:, :, 4:7, :], in0=win_b[:, :, 0:3 * CP].rearrange("p j (i c) -> p j i c", c=CP),
                    in1=centre.to_broadcast([P, KW, 3, CP]), op=ALU.subtract,
                )
            flat = diff[:].rearrange("p a f c -> p (a f c)")
            nc.scalar.activation(out=flat, in_=flat, func=ACT.Square)
            dst = affp.tile([P, 2 * (NOFF + 1)], F32, name="dst", tag="dst")
            nc.vector.tensor_reduce(out=dst[:], in_=diff[:].rearrange("p a f c -> p (a f) c"), axis=AX.X, op=ALU.add)
            gau = affp.tile([P, 2 * (NOFF + 1)], F32, name="gau", tag="gau")
            nc.scalar.activation(out=gau[:], in_=dst[:], func=ACT.Exp, scale=neginv[:, 0:1])
            ex = affp.tile([P, 2, NOFF + 1], F32, name="ex", tag="ex")
            nc.scalar.activation(out=ex[:].rearrange("p a f -> p (a f)"), in_=gau[:], func=ACT.Exp, bias=-1.0)
            em = affp.tile([P, 2, NOFF], F32, name="em", tag="em")
            nc.gpsimd.tensor_tensor(
                out=em[:], in0=ex[:, :, 0:NOFF],
                in1=mask49[:, 2 * pp:2 * pp + 2].rearrange("p t j i -> p t (j i)"), op=ALU.mult,
            )
            zs = affp.tile([P, 2], F32, name="zs", tag="zs")
            nc.vector.tensor_reduce(out=zs[:], in_=em[:], axis=AX.X, op=ALU.add)
            zo = affp.tile([P, 2], F32, name="zo", tag="zo")
            for a in range(2):
                nc.scalar.activation(
                    out=zo[:, a:a + 1], in_=ex[:, a, NOFF:NOFF + 1], func=ACT.Identity,
                    scale=cnt[:, 2 * pp + a:2 * pp + a + 1], bias=zs[:, a:a + 1],
                )
            rz = affp.tile([P, 2], F32, name="rz", tag="rz")
            nc.vector.reciprocal(out=rz[:], in_=zo[:])
            wa = affp.tile([P, 2, NOFF], F32, name="wa", tag="wa")
            for a in range(2):
                nc.scalar.activation(out=wa[:, a, :], in_=em[:, a, :], func=ACT.Copy, scale=rz[:, a:a + 1])
            later[("wa", pi)] = wa

        def stage2(n0, ag_flat):
            a_codes = work.tile([P, 2 * P], U32, name="a_codes", tag="a_codes", align_bytes=64)
            a_scl = work.tile([P, 2 * P], U8, name="a_scl", tag="a_scl", align_bytes=64)
            nc.vector.quantize_mx(out=a_codes[:].bitcast(FP8X4), scales=a_scl[:], in_=ag_flat)
            o_sb = work.tile([P, 4, 2 * P], F32, name="o_sb", tag="o_sb")
            for u in range(2):
                ps2 = ps_aux.tile([P, 2, 2 * P], F32, name="ps2", tag="aux")
                for h in range(2):
                    t = 2 * u + h
                    nc.tensor.matmul_mx(
                        out=ps2[:, h, :],
                        lhsT=later["wu"][0][:, P * t:P * t + P].bitcast(FP8X4), lhsT_scale=later["wu"][1][:, P * t:P * t + P],
                        rhs=a_codes[:].bitcast(FP8X4), rhs_scale=a_scl[:],
                        start=True, stop=True,
                    )
                nc.vector.tensor_tensor(
                    out=o_sb[:, 2 * u:2 * u + 2, :], in0=ps2[:], in1=x_raw[:, 2 * u:2 * u + 2, n0:n0 + 2 * P], op=ALU.add,
                )
            nc.sync.dma_start(out=out_v[:, :, n0:n0 + 2 * P], in_=o_sb[:])

        def e_begin(pi):
            later[("acc", pi)] = work.tile([P, 2, C], F32, name="acc_v", tag="acc_v")
            later[("acg", pi)] = work.tile([P, 2, C], F32, name="acc_g", tag="acc_g")

        def e_step(pi, f):
            acc = later[("acc", pi)]
            wa = later[("wa", pi)]
            djx, dix = divmod(f, KW)
            base = 2 * P * pi - ME0 + IMG_W * (dix - 3) + (djx - 3)
            src = msg_e if base % 2 == 0 else msg_o
            word0 = base // 2
            win = ps_win.tile([P, C], F32, name="win", tag="win")
            for t in range(4):
                nc.tensor.transpose(win[:, P * t:P * t + P], src[:, t, :].bitcast(F32)[:, word0:word0 + P], ident_f[:])
            halves = win[:].bitcast(BF16)
            acg = later[("acg", pi)]
            on_g = [i for i in range(NOFF) if i in g_set]
            first_g = f == min(on_g)
            first_v = f == min(i for i in range(NOFF) if i not in on_g)
            if f in on_g:
                prod = acg if first_g else work.tile([P, 2, C], F32, name="prod", tag="prod")
            for a in range(2):
                wcol = wa[:, a, f:f + 1]
                if f in on_g:
                    nc.scalar.activation(out=prod[:, a, :], in_=halves[:, a::2], func=ACT.Copy, scale=wcol)
                elif first_v:
                    nc.vector.tensor_scalar(out=acc[:, a, :], in0=halves[:, a::2], scalar1=wcol, scalar2=None, op0=ALU.mult)
                else:
                    nc.vector.scalar_tensor_tensor(
                        out=acc[:, a, :], in0=halves[:, a::2], scalar=wcol, in1=acc[:, a, :], op0=ALU.mult, op1=ALU.add,
                    )
            if f in on_g and not first_g:
                nc.gpsimd.tensor_tensor(out=acg[:], in0=acg[:], in1=prod[:], op=ALU.add)
            if f == NOFF - 1:
                nc.gpsimd.tensor_tensor(out=acg[:], in0=acg[:], in1=acc[:], op=ALU.add)

        def turn_back(pi, a):
            acc = later[("acg", pi)]
            if a == 0:
                later[("ag", pi)] = work.tile([P, 2 * P, 4], BF16, name="ag", tag="ag", align_bytes=64)
            back = ps_aux.tile([P, 4, P], F32, name="back", tag="aux")
            for t in range(4):
                nc.tensor.transpose(back[:, t, :], acc[:, a, P * t:P * t + P], ident_f[:])
            nc.scalar.copy(
                out=later[("ag", pi)][:].rearrange("p (n a) t -> p a n t", a=2)[:, a], in_=back[:].rearrange("p t n -> p n t"),
            )

        def e_stage2(pi):
            stage2(2 * P * pi, later[("ag", pi)][:].rearrange("p n t -> p (n t)"))

        plist = [(c, cb) for c in range(1, 10) for cb in range(8)]

        def p_front(idx):
            c, cb = plist[idx]
            pt = ps_pt.tile([P, 4, P], BF16, name="pt", tag="pt")
            for t in range(4):
                nc.tensor.transpose(pt[:, t, :], bands[:, cb, t, 48 * c - 12:48 * c - 12 + P], ident_b[:])
            pf = work.tile([P, 4, P], F32, name="pf", tag="pf", bufs=3)
            nc.scalar.copy(out=pf[:], in_=pt[:])
            later[("pf", idx)] = pf

        def p_back(idx):
            c, cb = plist[idx]
            half, cc = divmod(cb, 4)
            pf = later[("pf", idx)]
            if c == 1:
                nro = 7
                rhs = a_top[:, cb, :]
                if cc == 0:
                    for u in range(2):
                        later[("aggps", u)] = ps_agg.tile([P, 2, 7, NPOS], F32, name="aggtop", tag="agg")
            else:
                nro = 4 if c < 9 else (3 if cb < 3 else 2)
                rhs = a_sb[:, 9 * c + cb, 0:6 * nro]
                if cc == 0:
                    later[("aggps", 0)] = ps_agg.tile([P, 4, 4, NPOS], F32, name="aggps", tag="agg")
            for t in range(4):
                spot = later[("aggps", t // 2)][:, t % 2] if c == 1 else later[("aggps", 0)][:, t]
                nc.tensor.matmul(
                    out=spot[:, 0:nro, 6 * cc:6 * cc + 6], lhsT=pf[:, t, :],
                    rhs=rhs.rearrange("p (r c) -> p r c", c=6), start=True, stop=True,
                )
            if cc == 3:
                row0 = 0 if c == 1 else 4 * c - 1
                dst = ag_all[:, IMG_W * row0:IMG_W * (row0 + 7), :].rearrange("p (r w) t -> p r w t", w=IMG_W)
                if c == 1:
                    for u in range(2):
                        nc.scalar.copy(
                            out=dst[:, :, 24 * half:24 * half + 24, 2 * u:2 * u + 2],
                            in_=later[("aggps", u)][:].rearrange("p t r c -> p r c t"),
                        )
                else:
                    if c < 9:
                        pieces = [(0, 4, 24)]
                    elif half == 0:
                        pieces = [(0, 2, 24), (2, 3, 16)]
                    else:
                        pieces = [(0, 2, 24)]
                    for ra, rz_, ncol in pieces:
                        nc.scalar.copy(
                            out=dst[:, ra:rz_, 24 * half:24 * half + ncol, :],
                            in_=later[("aggps", 0)][:, :, ra:rz_, 0:ncol].rearrange("p t r c -> p r c t"),
                        )
                if half == 1:
                    ready = min(IMG_W * (4 * c + 3), PE_PIX)
                    while 256 * (later["chunk"] + 1) <= ready:
                        n0 = 256 * later["chunk"]
                        stage2(n0, ag_all[:, n0:n0 + 256, :].rearrange("p n t -> p (n t)"))
                        later["chunk"] = later["chunk"] + 1

        first, second = E_PAIRS
        stage1_quant(2)
        pz_build(0)
        a_group(0, 0)
        stage1_mm(2)
        affinity(first)
        e_begin(first)
        groups = [(0, 0), (0, 1), (1, 0), (1, 1), (2, 0), (2, 1)]
        for g, (bt, half) in enumerate(groups):
            if g > 0:
                a_group(bt, half)
            if half == 0 and bt < 2:
                pz_build(bt + 1)
            if half == 1:
                a_finish(bt)
            for f in range((g * HEAD_STEPS) // 6, ((g + 1) * HEAD_STEPS) // 6):
                e_step(first, f)
            if g == 1:
                stage1_quant(1)
            if g == 2:
                stage1_mm(1)
            if g == 4:
                later["wu"] = prep_weight(wu_raw, "wu")
        ag_all = work.tile([P, 2016, 4], BF16, name="ag_all", tag="big", align_bytes=64, bufs=1)
        later["chunk"] = 0

        e_items = []
        for f in range(HEAD_STEPS, NOFF):
            e_items.append(lambda f=f: e_step(first, f))
            if f == HEAD_STEPS + 4:
                e_items.append(lambda: affinity(second))
        e_items.append(lambda: e_begin(second))
        for f in range(NOFF):
            e_items.append(lambda f=f: e_step(second, f))
            if f == 1:
                e_items.append(lambda: turn_back(first, 0))
            if f == 3:
                e_items.append(lambda: turn_back(first, 1))
            if f == 6:
                e_items.append(lambda: e_stage2(first))
        e_items.append(lambda: turn_back(second, 0))
        e_items.append(lambda: turn_back(second, 1))
        e_items.append(lambda: e_stage2(second))

        n_e = len(e_items)
        done_e = 0
        for ip in range(len(plist) + 2):
            if ip < len(plist):
                p_front(ip)
            if ip >= 2:
                p_back(ip - 2)
            want = min(n_e, ((ip + 1) * n_e) // E_SPAN)
            while done_e < want:
                e_items[done_e]()
                done_e += 1
